import numpy as np
import ml_dtypes


def mxq(x, axis, fmt="e4m3"):
    dtype, down = {"e4m3": (ml_dtypes.float8_e4m3fn, 7), "e5m2": (ml_dtypes.float8_e5m2, 14)}[fmt]
    v = np.moveaxis(np.asarray(x, np.float32).astype(ml_dtypes.bfloat16).astype(np.float64), axis, -1)
    blocks = v.reshape(v.shape[:-1] + (-1, 32))
    amax = np.abs(blocks).max(-1, keepdims=True)
    byte = np.maximum(np.where(amax > 0, np.frexp(amax)[1] - 1 + 127, 0) - down, 1)
    scale = np.exp2(byte - 127.0)
    codes = (blocks / scale).astype(np.float32).astype(dtype).astype(np.float64)
    return np.moveaxis((codes * scale).reshape(v.shape), -1, axis)


WIDE = False


def mx_kscale(k):
    if not WIDE:
        return np.ones(k)
    levels = np.array([10, -10, 5, -5, 0])
    if k % 512:
        return np.exp2(np.random.permutation(np.resize(levels, k // 32))).repeat(32)
    a = np.empty((k // 512, 16))
    for p in range(k // 512):
        a[p, :8] = np.random.permutation(np.resize(levels, 8))
        for g in range(8):
            far = levels[np.abs(levels - a[p, g]) >= 10]
            a[p, g + 8] = far[np.random.randint(len(far))]
    return np.exp2(a.ravel()).repeat(32)


BF16 = ml_dtypes.bfloat16


def bf(x):
    return np.asarray(x, np.float32).astype(BF16)


def f64(x):
    return np.asarray(x).astype(np.float64)


B, S, E, H, D, F = 2, 256, 1024, 8, 128, 4096
EPS = 1e-6
QUIET = 3e-5
GELU_C = 0.7978845608028654
HD = H * D


def rmsnorm(x, scale):
    ms = np.mean(np.square(x), axis=-1, keepdims=True)
    return x * (1.0 / np.sqrt(ms + EPS)) * scale


def gelu_tanh(v):
    return 0.5 * v * (1.0 + np.tanh(GELU_C * (v + 0.044715 * v**3)))


def draw0():
    s, t = mx_kscale(HD), mx_kscale(E)
    amp = np.where(np.random.random((B, S, 1)) < 0.125, QUIET, 1.0)
    return {"attn": bf(np.random.standard_normal((B, S, H, D)) * 0.25 * amp[..., None] * s.reshape(H, D)),
            "x": bf(np.random.standard_normal((B, S, E)) * amp),
            "w_out": bf(np.random.standard_normal((H, D, E)) * 1.5 / np.sqrt(HD) / s.reshape(H, D, 1)),
            "scale2": bf(np.random.standard_normal(E) * t),
            "w_gate": bf(np.random.standard_normal((E, F)) / np.sqrt(E) / t[:, None]),
            "w_up": bf(np.random.standard_normal((E, F)) / np.sqrt(E) / t[:, None])}


def core(attn, x, w_out, scale2, w_gate, w_up):
    a = f64(attn).reshape(B * S, HD)
    h = f64(x).reshape(B * S, E) + (mxq(a, 1, "e4m3") @ mxq(f64(w_out).reshape(HD, E), 0, "e4m3"))
    hq = mxq(rmsnorm(h, f64(scale2)), 1, "e4m3")
    act = gelu_tanh(hq @ mxq(f64(w_gate), 0, "e4m3")) * (hq @ mxq(f64(w_up), 0, "e4m3"))
    return h.reshape(B, S, E), act.reshape(B, S, F)


def e4m3fn_bytes(y):
    return np.clip(np.asarray(y, np.float64), -448.0, 448.0).astype(np.float32).astype(ml_dtypes.float8_e4m3fn).view(np.uint8)


def e4m3fn_values(b):
    return np.asarray(b, np.uint8).view(ml_dtypes.float8_e4m3fn).astype(np.float64)


def setup_inputs():
    d = draw0()
    x0 = np.asarray(d['w_up']).astype(np.float64)
    s = (np.max(np.abs(x0), axis=(1,), keepdims=True) / 448.0).astype(np.float32)
    out = {}
    for k, v in d.items():
        if k == 'w_up':
            out['w_up_bytes'] = e4m3fn_bytes(x0 / s.astype(np.float64))
            out['w_up_scale'] = s
        else:
            out[k] = v
    return out


def reference(attn, x, w_out, scale2, w_gate, w_up_bytes, w_up_scale):
    return core(attn, x, w_out, scale2, w_gate, e4m3fn_values(w_up_bytes) * w_up_scale.astype(np.float64))

@@ -1,0 +1,229 @@
+from contextlib import ExitStack
+
+import concourse.mybir as mybir
+from concourse.masks import make_identity
+
+B, S, E, H, D, F = 2, 256, 1024, 8, 128, 4096
+EPS = 1e-6
+TOK = B * S
+HD = H * D
+P = 128
+G = 2
+M_TILES = TOK // P
+SUB = 512
+CHUNKS = F // SUB
+
+FLOPS = 2 * TOK * HD * E + 2 * 2 * TOK * E * F
+
+F32 = mybir.dt.float32
+BF16 = mybir.dt.bfloat16
+U32 = mybir.dt.uint32
+U8 = mybir.dt.uint8
+FP8 = mybir.dt.float8_e4m3fn
+FP8X4 = mybir.dt.float8_e4m3fn_x4
+ALU = mybir.AluOpType
+ACT = mybir.ActivationFunctionType
+
+
+def tile_block_pb_kernel(tc, attn, x, w_out, scale2, w_gate, w_up_bytes, w_up_scale, h_out, act_out):
+    nc = tc.nc
+    attn_v = attn.rearrange("b s h d -> (b s) (h d)").rearrange("(m p) k -> p m k", p=P)
+    x_v = x.rearrange("b s e -> (b s) e").rearrange("(m p) e -> p m e", p=P)
+    wo_v = w_out.rearrange("h d e -> (h d) e").rearrange("(g p t) n -> g p t n", p=P, t=4)
+    gate_v = w_gate.rearrange("(g p t) n -> g p t n", p=P, t=4)
+    up_v = w_up_bytes.rearrange("(g p t) n -> g p t n", p=P, t=4)
+    upscale_v = w_up_scale.rearrange("(g p t) o -> p g (t o)", p=P, t=4)
+    h_v = h_out.rearrange("b s e -> (b s) e").rearrange("(m p) e -> m p e", p=P)
+    act_v = act_out.rearrange("b s f -> (b s) f").rearrange("(m p) f -> m p f", p=P)
+
+    with ExitStack() as ctx:
+        keep = ctx.enter_context(tc.tile_pool(name="keep", bufs=1))
+        load = ctx.enter_context(tc.tile_pool(name="load", bufs=1))
+        work = ctx.enter_context(tc.tile_pool(name="work", bufs=1))
+        psum = ctx.enter_context(tc.psum_pool(name="psum", bufs=8))
+
+        dummy = keep.tile([P, 1], F32)
+        nc.vector.memset(dummy[:], 0.0)
+        dummy2 = keep.tile([P, 1], F32)
+        nc.scalar.activation(out=dummy2[:], in_=dummy[:], func=ACT.Gelu_apprx_tanh)
+        s2row = keep.tile([P, E], BF16)
+        nc.gpsimd.memset(s2row[:].bitcast(F32), 0.0)
+        nc.gpsimd.dma_start(out=s2row[0:1, :], in_=scale2.rearrange("(o e) -> o e", o=1))
+        ones = keep.tile([P, P], BF16)
+        nc.gpsimd.memset(ones[:], 1.0)
+        ident = keep.tile([P, P], F32)
+        make_identity(nc, ident[:])
+        neghalf = keep.tile([P, 1], F32)
+        nc.gpsimd.memset(neghalf[:], -0.5)
+        upscale = keep.tile([P, G, 4], F32)
+        nc.scalar.dma_start(out=upscale[:], in_=upscale_v)
+
+        wo_raw = {}
+        at_raw = []
+        x_raw = []
+
+        def load_wo(g, n):
+            t = load.tile([P, 4, SUB], BF16, name="wo_raw", bufs=4)
+            nc.sync.dma_start(out=t[:], in_=wo_v[g][:, :, n * SUB:(n + 1) * SUB])
+            wo_raw[g, n] = t
+
+        def load_at(i):
+            t = load.tile([P, 2, HD], BF16, name="at_raw", bufs=2)
+            nc.sync.dma_start(out=t[:], in_=attn_v[:, 2 * i:2 * i + 2, :])
+            at_raw.append(t)
+
+        def load_x(i):
+            t = load.tile([P, 2, E], BF16, name="x_raw", bufs=2)
+            nc.sync.dma_start(out=t[:], in_=x_v[:, 2 * i:2 * i + 2, :])
+            x_raw.append(t)
+
+        gate_raw = {}
+        up_raw = {}
+
+        def load_gate(g, c):
+            t = load.tile([P, 4, 2 * SUB], BF16, name="gate_raw", bufs=5)
+            nc.sync.dma_start(out=t[:], in_=gate_v[g][:, :, c * 2 * SUB:(c + 1) * 2 * SUB])
+            gate_raw[g, c] = t
+
+        def load_up(g, c):
+            t = load.tile([P, 4, 2 * SUB], U8, name="up_raw", bufs=6)
+            nc.sync.dma_start(out=t[:], in_=up_v[g][:, :, c * 2 * SUB:(c + 1) * 2 * SUB])
+            up_raw[g, c] = t
+
+        load_wo(0, 0)
+        load_at(0)
+        load_wo(0, 1)
+        load_at(1)
+        load_up(0, 0)
+        load_wo(1, 0)
+        load_wo(1, 1)
+        load_x(0)
+        load_gate(0, 0)
+        load_x(1)
+        load_gate(1, 0)
+        load_up(1, 0)
+
+        def interleave(copy, src):
+            dst = work.tile([P, 4 * SUB], BF16, name="il", bufs=4, align_bytes=64)
+            copy(
+                out=dst[:].rearrange("p (c i t) -> p c t i", i=4, t=4),
+                in_=src.rearrange("p t (c i) -> p c t i", i=4),
+            )
+            return dst
+
+        def new_codes():
+            codes = work.tile([P, G, SUB], U32, name="codes", bufs=11, align_bytes=64)
+            scales = work.tile([P, G, SUB], U8, name="scales", bufs=11, align_bytes=64)
+            return codes, scales
+
+        def quantize(cs, g, src):
+            nc.vector.quantize_mx(out=cs[0][:, g, :].bitcast(FP8X4), scales=cs[1][:, g, :], in_=src[:])
+
+        def turn(words, codes, scales, m):
+            bank = psum.tile([P, G, 2, P], F32, name="bank")
+            for g in range(G):
+                for u in range(2):
+                    nc.tensor.transpose(bank[:, g, u, :], words[:, 256 * g + u:256 * (g + 1):2], ident[:])
+            grouped = work.tile([P, G * P * 4], BF16, name="grouped", bufs=2, align_bytes=64)
+            nc.scalar.copy(
+                out=grouped[:].bitcast(F32).rearrange("p (g r u) -> p g r u", g=G, u=2),
+                in_=bank[:].rearrange("p g u r -> p g r u"),
+            )
+            nc.vector.quantize_mx(
+                out=codes[:, m, :].bitcast(FP8X4), scales=scales[:, m, :], in_=grouped[:]
+            )
+
+        def mm(bank, lhs, m, rhs):
+            for g in range(G):
+                nc.tensor.matmul_mx(
+                    out=bank[:],
+                    lhsT=lhs[0][:, m, g * P:(g + 1) * P].bitcast(FP8X4),
+                    lhsT_scale=lhs[1][:, m, g * P:(g + 1) * P],
+                    rhs=rhs[0][:, g, :].bitcast(FP8X4),
+                    rhs_scale=rhs[1][:, g, :],
+                    start=(g == 0),
+                    stop=(g == G - 1),
+                )
+
+        s2b = keep.tile([P, E], BF16)
+        for n in range(2):
+            bank = psum.tile([P, SUB], F32, name="bank")
+            nc.tensor.matmul(bank[:], lhsT=ones[:], rhs=s2row[:, n * SUB:(n + 1) * SUB], start=True, stop=True)
+            nc.scalar.copy(out=s2b[:, n * SUB:(n + 1) * SUB], in_=bank[:])
+
+        at_codes = keep.tile([P, M_TILES, G * P], U32, align_bytes=64)
+        at_scales = keep.tile([P, M_TILES, G * P], U8, align_bytes=64)
+        at = (at_codes, at_scales)
+        wo = [new_codes(), new_codes()]
+        for m in range(M_TILES):
+            turn(at_raw[m // 2][:, m % 2, :].bitcast(F32), at_codes, at_scales, m)
+            g, n = m // 2, m % 2
+            quantize(wo[n], g, interleave(nc.vector.tensor_copy, wo_raw[g, n][:]))
+
+        hn_codes = keep.tile([P, M_TILES, G * P], U32, align_bytes=64)
+        hn_scales = keep.tile([P, M_TILES, G * P], U8, align_bytes=64)
+        hn_q = (hn_codes, hn_scales)
+        ms = keep.tile([P, 8 * M_TILES], F32)
+        for m in range(M_TILES):
+            h = work.tile([P, E], F32, name="h", bufs=2)
+            for n in range(2):
+                bank = psum.tile([P, SUB], F32, name="bank")
+                mm(bank, at, m, wo[n])
+                cols = slice(n * SUB, (n + 1) * SUB)
+                nc.vector.tensor_tensor(out=h[:, cols], in0=bank[:], in1=x_raw[m // 2][:, m % 2, cols], op=ALU.add)
+            nc.sync.dma_start(out=h_v[m], in_=h[:])
+            junk = work.tile([P, E], F32, name="junk", bufs=1)
+            stat = work.tile([P, 8], F32, name="stat", bufs=2)
+            var = work.tile([P, 8], F32, name="var", bufs=2)
+            rstd = work.tile([P, 8], F32, name="rstd", bufs=2)
+            nc.scalar.activation(out=junk[:], in_=h[:], func=ACT.Square, scale=1.0 / 32.0, accum_out=stat[:, 0:1])
+            nc.gpsimd.tensor_scalar(out=var[:, 0:1], in0=stat[:, 0:1], scalar1=1.0, scalar2=EPS, op0=ALU.mult, op1=ALU.add)
+            nc.gpsimd.tensor_tensor(out=rstd[:, 0:1], in0=var[:, 0:1], in1=neghalf[:], op=ALU.pow)
+            hn = work.tile([P, E], BF16, name="hn", bufs=2)
+            nc.vector.scalar_tensor_tensor(
+                out=hn[:], in0=h[:], scalar=rstd[:, 0:1], in1=s2b[:], op0=ALU.mult, op1=ALU.mult
+            )
+            turn(hn[:].bitcast(F32), hn_codes, hn_scales, m)
+
+        gate_q = {}
+        up_q = {}
+
+        def prep(c):
+            half = slice((c % 2) * SUB, (c % 2 + 1) * SUB)
+            gate_q[c] = new_codes()
+            up_q[c] = new_codes()
+            for g in range(G):
+                copy = nc.scalar.copy if g == 1 else nc.vector.tensor_copy
+                quantize(gate_q[c], g, interleave(copy, gate_raw[g, c // 2][:, :, half]))
+                wide = work.tile([P, 4, SUB], BF16, name="wide", bufs=3)
+                for t in range(4):
+                    nc.scalar.activation(
+                        out=wide[:, t, :],
+                        in_=up_raw[g, c // 2][:, t, half].bitcast(FP8),
+                        func=ACT.Copy,
+                        scale=upscale[:, g, t:t + 1],
+                    )
+                quantize(up_q[c], g, interleave(nc.vector.tensor_copy, wide[:]))
+
+        def outputs(c):
+            for m in range(M_TILES):
+                gbank = psum.tile([P, SUB], F32, name="bank")
+                mm(gbank, hn_q, m, gate_q[c])
+                ubank = psum.tile([P, SUB], F32, name="bank")
+                mm(ubank, hn_q, m, up_q[c])
+                gel = work.tile([P, SUB], F32, name="gel", bufs=3)
+                nc.scalar.activation(out=gel[:], in_=gbank[:], func=ACT.Gelu_apprx_tanh)
+                res = work.tile([P, SUB], F32, name="res", bufs=4)
+                nc.vector.tensor_tensor(out=res[:], in0=ubank[:], in1=gel[:], op=ALU.mult)
+                nc.sync.dma_start(out=act_v[m][:, c * SUB:(c + 1) * SUB], in_=res[:])
+
+        prep(0)
+        for c in range(1, CHUNKS):
+            if c % 2 == 0:
+                load_gate(0, c // 2)
+                load_up(0, c // 2)
+                load_gate(1, c // 2)
+                load_up(1, c // 2)
+            prep(c)
+            outputs(c - 1)
+        outputs(CHUNKS - 1)

@@ -15,6 +15,26 @@ CHUNKS = F // SUB
 
 FLOPS = 2 * TOK * HD * E + 2 * 2 * TOK * E * F
 
+GATE_BUFS = 4
+UP_BUFS = 6
+WIDE_BUFS = 3
+IL_BUFS = 5
+CODE_BUFS = 10
+SHARE = "PE"
+AHEAD = 3
+NB1 = 2
+NB2 = 1
+LAST = 28
+BY_PASS = 1
+ORD = ["gate","up"]
+ML = 2
+GL = 2
+GFIRST = 0
+NB0 = 0
+RES_BUFS = 6
+SH0 = 3
+VW = 9
+
 F32 = mybir.dt.float32
 BF16 = mybir.dt.bfloat16
 U32 = mybir.dt.uint32
@@ -37,101 +57,210 @@ def tile_block_pb_kernel(tc, attn, x, w_out, scale2, w_gate, w_up_bytes, w_up_sc
     act_v = act_out.rearrange("b s f -> (b s) f").rearrange("(m p) f -> m p f", p=P)
 
     with ExitStack() as ctx:
+        ctx.enter_context(tc.manual_schedule())
         keep = ctx.enter_context(tc.tile_pool(name="keep", bufs=1))
         load = ctx.enter_context(tc.tile_pool(name="load", bufs=1))
         work = ctx.enter_context(tc.tile_pool(name="work", bufs=1))
         psum = ctx.enter_context(tc.psum_pool(name="psum", bufs=8))
 
+        wo_raw = {}
+        at_raw = {}
+        x_raw = {}
+        gate_raw = {}
+        up_raw = {}
+
+        def load_wo(g, n):
+            wo_raw[g, n] = load.tile([P, 4, SUB], BF16, name="wo_raw", bufs=4)
+            nc.sync.dma_start(out=wo_raw[g, n][:], in_=wo_v[g][:, :, n * SUB:(n + 1) * SUB])
+
+        def load_at(i):
+            at_raw[i] = load.tile([P, 2, HD], BF16, name="at_raw", bufs=2)
+            nc.sync.dma_start(out=at_raw[i][:], in_=attn_v[:, 2 * i:2 * i + 2, :])
+
+        def load_x(i):
+            x_raw[i] = load.tile([P, 2, E], BF16, name="x_raw", bufs=2)
+            nc.sync.dma_start(out=x_raw[i][:], in_=x_v[:, 2 * i:2 * i + 2, :])
+
+        def load_gate(g, c):
+            gate_raw[g, c] = load.tile([P, 4, 2 * SUB], BF16, name="gate_raw", bufs=GATE_BUFS)
+            nc.sync.dma_start(out=gate_raw[g, c][:], in_=gate_v[g][:, :, c * 2 * SUB:(c + 1) * 2 * SUB])
+
+        def load_up(g, c):
+            up_raw[g, c] = load.tile([P, 4, 2 * SUB], U8, name="up_raw", bufs=UP_BUFS)
+            nc.sync.dma_start(out=up_raw[g, c][:], in_=up_v[g][:, :, c * 2 * SUB:(c + 1) * 2 * SUB])
+
+        load_wo(0, 0)
+        load_up(0, 0)
+        load_wo(0, 1)
+        load_at(0)
+        load_wo(1, 0)
+        load_at(1)
+        load_wo(1, 1)
+        load_gate(0, 0)
+        load_x(0)
+        load_up(1, 0)
+        load_x(1)
+        load_gate(1, 0)
+        load_up(0, 1)
+        load_up(1, 1)
+        load_gate(0, 1)
+        load_gate(1, 1)
+
         dummy = keep.tile([P, 1], F32)
         nc.vector.memset(dummy[:], 0.0)
         dummy2 = keep.tile([P, 1], F32)
         nc.scalar.activation(out=dummy2[:], in_=dummy[:], func=ACT.Gelu_apprx_tanh)
+        upscale = keep.tile([P, G, 4], F32)
+        nc.scalar.dma_start(out=upscale[:], in_=upscale_v)
+        ident = keep.tile([P, P], F32)
+        make_identity(nc, ident[:])
         s2row = keep.tile([P, E], BF16)
         nc.gpsimd.memset(s2row[:].bitcast(F32), 0.0)
         nc.gpsimd.dma_start(out=s2row[0:1, :], in_=scale2.rearrange("(o e) -> o e", o=1))
         ones = keep.tile([P, P], BF16)
         nc.gpsimd.memset(ones[:], 1.0)
-        ident = keep.tile([P, P], F32)
-        make_identity(nc, ident[:])
+        ident_bf = keep.tile([P, P], BF16)
+        nc.vector.tensor_copy(out=ident_bf[:], in_=ident[:])
         neghalf = keep.tile([P, 1], F32)
         nc.gpsimd.memset(neghalf[:], -0.5)
-        upscale = keep.tile([P, G, 4], F32)
-        nc.scalar.dma_start(out=upscale[:], in_=upscale_v)
 
-        wo_raw = {}
-        at_raw = []
-        x_raw = []
+        units = []
+        for g in range(G):
+            for n in range(2):
+                units.append(("wo", n, g))
+        for c in range(0, CHUNKS, 2):
+            pair = [(c, g) for g in range(G)] + [(c + 1, g) for g in range(G)]
+            if c < 2 * BY_PASS:
+                pair = [(d, g) for g in range(G) for d in (c, c + 1)]
+            for d, g in pair:
+                units.append((ORD[0], d, g))
+                units.append((ORD[1], d, g))
+        codes = {}
+        grouped = {}
+        wide = {}
+        state = {"ahead": 0, "il": 0, "q": 0, "load": 2}
 
-        def load_wo(g, n):
-            t = load.tile([P, 4, SUB], BF16, name="wo_raw", bufs=4)
-            nc.sync.dma_start(out=t[:], in_=wo_v[g][:, :, n * SUB:(n + 1) * SUB])
-            wo_raw[g, n] = t
+        def source(u):
+            kind, c, g = u
+            if kind == "wo":
+                return wo_raw[g, c][:]
+            if kind == "gate":
+                return gate_raw[g, c // 2][:, :, (c % 2) * SUB:(c % 2 + 1) * SUB]
+            return wide[u][:]
 
-        def load_at(i):
-            t = load.tile([P, 2, HD], BF16, name="at_raw", bufs=2)
-            nc.sync.dma_start(out=t[:], in_=attn_v[:, 2 * i:2 * i + 2, :])
-            at_raw.append(t)
+        def vwiden(u):
+            return u[0] == "up" and u[2] == 1 and u[1] % VW == VW - 1
 
-        def load_x(i):
-            t = load.tile([P, 2, E], BF16, name="x_raw", bufs=2)
-            nc.sync.dma_start(out=t[:], in_=x_v[:, 2 * i:2 * i + 2, :])
-            x_raw.append(t)
+        def widen(u):
+            kind, c, g = u
+            wide[u] = work.tile([P, 4, SUB], BF16, name="wide", bufs=WIDE_BUFS)
+            half = slice((c % 2) * SUB, (c % 2 + 1) * SUB)
+            for t in range(4):
+                if vwiden(u):
+                    nc.vector.tensor_scalar(
+                        out=wide[u][:, t, :],
+                        in0=up_raw[g, c // 2][:, t, half].bitcast(FP8),
+                        scalar1=upscale[:, g, t:t + 1],
+                        scalar2=None,
+                        op0=ALU.mult,
+                    )
+                    continue
+                nc.scalar.activation(
+                    out=wide[u][:, t, :],
+                    in_=up_raw[g, c // 2][:, t, half].bitcast(FP8),
+                    func=ACT.Copy,
+                    scale=upscale[:, g, t:t + 1],
+                )
 
-        gate_raw = {}
-        up_raw = {}
+        def il(u, engine):
+            src = source(u)
+            dst = work.tile([P, 4 * SUB], BF16, name="il", bufs=IL_BUFS, align_bytes=64)
+            grouped[u] = dst
+            if engine == "PE":
+                for b in range(2):
+                    bank = psum.tile([P, 2 * SUB], BF16, name="bank")
+                    for q in range(2):
+                        c0 = (2 * b + q) * P
+                        nc.tensor.matmul(
+                            bank[:, q * SUB:(q + 1) * SUB],
+                            lhsT=ident_bf[:],
+                            rhs=src[:, :, c0:c0 + P].rearrange("p t c -> p c t"),
+                            start=True,
+                            stop=True,
+                        )
+                    nc.scalar.copy(out=dst[:, b * 2 * SUB:(b + 1) * 2 * SUB], in_=bank[:])
+            else:
+                copy = nc.vector.tensor_copy if engine == "V" else nc.scalar.copy
+                copy(
+                    out=dst[:].rearrange("p (c i t) -> p c t i", i=4, t=4),
+                    in_=src.rearrange("p t (c i) -> p c t i", i=4),
+                )
 
-        def load_gate(g, c):
-            t = load.tile([P, 4, 2 * SUB], BF16, name="gate_raw", bufs=5)
-            nc.sync.dma_start(out=t[:], in_=gate_v[g][:, :, c * 2 * SUB:(c + 1) * 2 * SUB])
-            gate_raw[g, c] = t
+        def quant():
+            u = units[state["q"]]
+            state["q"] += 1
+            kind, c, g = u
+            if g == 0:
+                codes[kind, c] = (
+                    work.tile([P, G, SUB], U32, name="codes", bufs=CODE_BUFS, align_bytes=64),
+                    work.tile([P, G, SUB], U8, name="scales", bufs=CODE_BUFS, align_bytes=64),
+                )
+            cd, sc = codes[kind, c]
+            nc.vector.quantize_mx(out=cd[:, g, :].bitcast(FP8X4), scales=sc[:, g, :], in_=grouped.pop(u)[:])
 
-        def load_up(g, c):
-            t = load.tile([P, 4, 2 * SUB], U8, name="up_raw", bufs=6)
-            nc.sync.dma_start(out=t[:], in_=up_v[g][:, :, c * 2 * SUB:(c + 1) * 2 * SUB])
-            up_raw[g, c] = t
+        def engine_of(u):
+            kind, c, g = u
+            return SHARE if kind == "gate" and (g == 1 or c % SH0 == SH0 - 1) else "V"
 
-        load_wo(0, 0)
-        load_at(0)
-        load_wo(0, 1)
-        load_at(1)
-        load_up(0, 0)
-        load_wo(1, 0)
-        load_wo(1, 1)
-        load_x(0)
-        load_gate(0, 0)
-        load_x(1)
-        load_gate(1, 0)
-        load_up(1, 0)
+        def s_ahead(to):
+            while state["ahead"] < min(to, len(units)):
+                u = units[state["ahead"]]
+                state["ahead"] += 1
+                if u[0] == "up" and not vwiden(u):
+                    widen(u)
+                if engine_of(u) != "V":
+                    il(u, engine_of(u))
 
-        def interleave(copy, src):
-            dst = work.tile([P, 4 * SUB], BF16, name="il", bufs=4, align_bytes=64)
-            copy(
-                out=dst[:].rearrange("p (c i t) -> p c t i", i=4, t=4),
-                in_=src.rearrange("p t (c i) -> p c t i", i=4),
-            )
-            return dst
+        def prep(ahead=None):
+            i = state["il"]
+            if i in (4 + 8 - 2, 4 + 16 - 2):
+                load_more()
+            s_ahead(i + 1 + (AHEAD if ahead is None else ahead))
+            if i < len(units):
+                state["il"] += 1
+                if vwiden(units[i]):
+                    widen(units[i])
+                if engine_of(units[i]) == "V":
+                    il(units[i], "V")
+            if state["q"] < state["il"] - (1 if i < len(units) else 0):
+                quant()
 
-        def new_codes():
-            codes = work.tile([P, G, SUB], U32, name="codes", bufs=11, align_bytes=64)
-            scales = work.tile([P, G, SUB], U8, name="scales", bufs=11, align_bytes=64)
-            return codes, scales
+        def load_more():
+            c = state["load"]
+            if c < 4:
+                state["load"] += 1
+                load_gate(0, c)
+                load_up(0, c)
+                load_gate(1, c)
+                load_up(1, c)
 
-        def quantize(cs, g, src):
-            nc.vector.quantize_mx(out=cs[0][:, g, :].bitcast(FP8X4), scales=cs[1][:, g, :], in_=src[:])
-
-        def turn(words, codes, scales, m):
+        def turn_pe(words):
             bank = psum.tile([P, G, 2, P], F32, name="bank")
             for g in range(G):
                 for u in range(2):
                     nc.tensor.transpose(bank[:, g, u, :], words[:, 256 * g + u:256 * (g + 1):2], ident[:])
-            grouped = work.tile([P, G * P * 4], BF16, name="grouped", bufs=2, align_bytes=64)
+            return bank
+
+        def turn_copy(bank):
+            t = work.tile([P, G * P * 4], BF16, name="turned", bufs=2, align_bytes=64)
             nc.scalar.copy(
-                out=grouped[:].bitcast(F32).rearrange("p (g r u) -> p g r u", g=G, u=2),
+                out=t[:].bitcast(F32).rearrange("p (g r u) -> p g r u", g=G, u=2),
                 in_=bank[:].rearrange("p g u r -> p g r u"),
             )
-            nc.vector.quantize_mx(
-                out=codes[:, m, :].bitcast(FP8X4), scales=scales[:, m, :], in_=grouped[:]
-            )
+            return t
+
+        def turn_quant(t, dst, m):
+            nc.vector.quantize_mx(out=dst[0][:, m, :].bitcast(FP8X4), scales=dst[1][:, m, :], in_=t[:])
 
         def mm(bank, lhs, m, rhs):
             for g in range(G):
@@ -145,85 +274,129 @@ def tile_block_pb_kernel(tc, attn, x, w_out, scale2, w_gate, w_up_bytes, w_up_sc
                     stop=(g == G - 1),
                 )
 
+        at_codes = keep.tile([P, M_TILES, G * P], U32, align_bytes=64)
+        at_scales = keep.tile([P, M_TILES, G * P], U8, align_bytes=64)
+        at_q = (at_codes, at_scales)
+        hn_codes = keep.tile([P, M_TILES, G * P], U32, align_bytes=64)
+        hn_scales = keep.tile([P, M_TILES, G * P], U8, align_bytes=64)
+        hn_q = (hn_codes, hn_scales)
+
+        turned = {}
+        prep(0)
+        s_ahead(6)
+        prep()
+        prep()
+        for m in range(M_TILES):
+            turned[m] = turn_copy(turn_pe(at_raw[m // 2][:, m % 2, :].bitcast(F32)))
+            if m == 1:
+                prep()
+            if m > 0:
+                turn_quant(turned.pop(m - 1), at_q, m - 1)
+        prep()
+        turn_quant(turned.pop(3), at_q, 3)
         s2b = keep.tile([P, E], BF16)
         for n in range(2):
             bank = psum.tile([P, SUB], F32, name="bank")
             nc.tensor.matmul(bank[:], lhsT=ones[:], rhs=s2row[:, n * SUB:(n + 1) * SUB], start=True, stop=True)
             nc.scalar.copy(out=s2b[:, n * SUB:(n + 1) * SUB], in_=bank[:])
 
-        at_codes = keep.tile([P, M_TILES, G * P], U32, align_bytes=64)
-        at_scales = keep.tile([P, M_TILES, G * P], U8, align_bytes=64)
-        at = (at_codes, at_scales)
-        wo = [new_codes(), new_codes()]
-        for m in range(M_TILES):
-            turn(at_raw[m // 2][:, m % 2, :].bitcast(F32), at_codes, at_scales, m)
-            g, n = m // 2, m % 2
-            quantize(wo[n], g, interleave(nc.vector.tensor_copy, wo_raw[g, n][:]))
+        h_banks = {}
+        h_t = {}
+        r_t = {}
 
-        hn_codes = keep.tile([P, M_TILES, G * P], U32, align_bytes=64)
-        hn_scales = keep.tile([P, M_TILES, G * P], U8, align_bytes=64)
-        hn_q = (hn_codes, hn_scales)
-        ms = keep.tile([P, 8 * M_TILES], F32)
-        for m in range(M_TILES):
-            h = work.tile([P, E], F32, name="h", bufs=2)
+        def h_mm(m):
             for n in range(2):
-                bank = psum.tile([P, SUB], F32, name="bank")
-                mm(bank, at, m, wo[n])
+                h_banks[m, n] = psum.tile([P, SUB], F32, name="bank")
+                mm(h_banks[m, n], at_q, m, codes["wo", n])
+
+        def h_add(m):
+            h_t[m] = work.tile([P, E], F32, name="h", bufs=2)
+            for n in range(2):
                 cols = slice(n * SUB, (n + 1) * SUB)
-                nc.vector.tensor_tensor(out=h[:, cols], in0=bank[:], in1=x_raw[m // 2][:, m % 2, cols], op=ALU.add)
-            nc.sync.dma_start(out=h_v[m], in_=h[:])
+                nc.vector.tensor_tensor(
+                    out=h_t[m][:, cols], in0=h_banks.pop((m, n))[:], in1=x_raw[m // 2][:, m % 2, cols], op=ALU.add
+                )
+            nc.sync.dma_start(out=h_v[m], in_=h_t[m][:])
+
+        def h_stat(m):
             junk = work.tile([P, E], F32, name="junk", bufs=1)
             stat = work.tile([P, 8], F32, name="stat", bufs=2)
             var = work.tile([P, 8], F32, name="var", bufs=2)
-            rstd = work.tile([P, 8], F32, name="rstd", bufs=2)
-            nc.scalar.activation(out=junk[:], in_=h[:], func=ACT.Square, scale=1.0 / 32.0, accum_out=stat[:, 0:1])
+            r_t[m] = work.tile([P, 8], F32, name="rstd", bufs=2)
+            nc.scalar.activation(out=junk[:], in_=h_t[m][:], func=ACT.Square, scale=1.0 / 32.0, accum_out=stat[:, 0:1])
             nc.gpsimd.tensor_scalar(out=var[:, 0:1], in0=stat[:, 0:1], scalar1=1.0, scalar2=EPS, op0=ALU.mult, op1=ALU.add)
-            nc.gpsimd.tensor_tensor(out=rstd[:, 0:1], in0=var[:, 0:1], in1=neghalf[:], op=ALU.pow)
+            nc.gpsimd.tensor_tensor(out=r_t[m][:, 0:1], in0=var[:, 0:1], in1=neghalf[:], op=ALU.pow)
+
+        def h_norm(m):
             hn = work.tile([P, E], BF16, name="hn", bufs=2)
             nc.vector.scalar_tensor_tensor(
-                out=hn[:], in0=h[:], scalar=rstd[:, 0:1], in1=s2b[:], op0=ALU.mult, op1=ALU.mult
+                out=hn[:], in0=h_t.pop(m)[:], scalar=r_t.pop(m)[:, 0:1], in1=s2b[:], op0=ALU.mult, op1=ALU.mult
             )
-            turn(hn[:].bitcast(F32), hn_codes, hn_scales, m)
+            return hn
 
-        gate_q = {}
-        up_q = {}
+        gb = {}
+        ub = {}
+        gel = {}
 
-        def prep(c):
-            half = slice((c % 2) * SUB, (c % 2 + 1) * SUB)
-            gate_q[c] = new_codes()
-            up_q[c] = new_codes()
-            for g in range(G):
-                copy = nc.scalar.copy if g == 1 else nc.vector.tensor_copy
-                quantize(gate_q[c], g, interleave(copy, gate_raw[g, c // 2][:, :, half]))
-                wide = work.tile([P, 4, SUB], BF16, name="wide", bufs=3)
-                for t in range(4):
-                    nc.scalar.activation(
-                        out=wide[:, t, :],
-                        in_=up_raw[g, c // 2][:, t, half].bitcast(FP8),
-                        func=ACT.Copy,
-                        scale=upscale[:, g, t:t + 1],
-                    )
-                quantize(up_q[c], g, interleave(nc.vector.tensor_copy, wide[:]))
+        def out_mm(j):
+            c, m = divmod(j, M_TILES)
+            last = max(units.index(("gate", c, 1)), units.index(("up", c, 1)))
+            while state["q"] <= last:
+                prep()
+            gb[j] = psum.tile([P, SUB], F32, name="bank")
+            mm(gb[j], hn_q, m, codes["gate", c])
+            ub[j] = psum.tile([P, SUB], F32, name="bank")
+            mm(ub[j], hn_q, m, codes["up", c])
 
-        def outputs(c):
-            for m in range(M_TILES):
-                gbank = psum.tile([P, SUB], F32, name="bank")
-                mm(gbank, hn_q, m, gate_q[c])
-                ubank = psum.tile([P, SUB], F32, name="bank")
-                mm(ubank, hn_q, m, up_q[c])
-                gel = work.tile([P, SUB], F32, name="gel", bufs=3)
-                nc.scalar.activation(out=gel[:], in_=gbank[:], func=ACT.Gelu_apprx_tanh)
-                res = work.tile([P, SUB], F32, name="res", bufs=4)
-                nc.vector.tensor_tensor(out=res[:], in0=ubank[:], in1=gel[:], op=ALU.mult)
-                nc.sync.dma_start(out=act_v[m][:, c * SUB:(c + 1) * SUB], in_=res[:])
+        def out_gelu(j):
+            gel[j] = work.tile([P, SUB], F32, name="gel", bufs=GL + 2)
+            nc.scalar.activation(out=gel[j][:], in_=gb.pop(j)[:], func=ACT.Gelu_apprx_tanh)
 
-        prep(0)
-        for c in range(1, CHUNKS):
-            if c % 2 == 0:
-                load_gate(0, c // 2)
-                load_up(0, c // 2)
-                load_gate(1, c // 2)
-                load_up(1, c // 2)
-            prep(c)
-            outputs(c - 1)
-        outputs(CHUNKS - 1)
+        def out_mul(j):
+            c, m = divmod(j, M_TILES)
+            res = work.tile([P, SUB], F32, name="res", bufs=RES_BUFS)
+            nc.vector.tensor_tensor(out=res[:], in0=ub.pop(j)[:], in1=gel.pop(j)[:], op=ALU.mult)
+            nc.sync.dma_start(out=act_v[m][:, c * SUB:(c + 1) * SUB], in_=res[:])
+
+        h_mm(0)
+        h_mm(1)
+        for i in range(M_TILES + 2):
+            if i < M_TILES:
+                h_add(i)
+                h_stat(i)
+            for n in range(NB1 + (i == 0) * NB0):
+                prep()
+            if 1 <= i <= M_TILES:
+                hn = h_norm(i - 1)
+                bank = turn_pe(hn[:].bitcast(F32))
+                turned[i - 1] = turn_copy(bank)
+            if i + 2 < M_TILES:
+                h_mm(i + 2)
+            for n in range(NB2):
+                prep()
+            if 2 <= i:
+                turn_quant(turned.pop(i - 2), hn_q, i - 2)
+
+        steps = CHUNKS * M_TILES
+        first = state["il"]
+        for j in range(ML):
+            out_mm(j)
+        for j in range(GL):
+            out_gelu(j)
+        for j in range(steps):
+            if GFIRST:
+                if j + ML < steps:
+                    out_mm(j + ML)
+                if j + GL < steps:
+                    out_gelu(j + GL)
+            want = first + ((j + 1) * (len(units) - first) + LAST - 1) // LAST
+            while state["il"] < min(want, len(units)):
+                prep()
+            if state["il"] == len(units) and state["q"] < len(units):
+                prep()
+            if not GFIRST:
+                if j + ML < steps:
+                    out_mm(j + ML)
+                if j + GL < steps:
+                    out_gelu(j + GL)
+            out_mul(j)

@@ -15,25 +15,33 @@ CHUNKS = F // SUB
 
 FLOPS = 2 * TOK * HD * E + 2 * 2 * TOK * E * F
 
-GATE_BUFS = 4
+GATE_BUFS = 5
 UP_BUFS = 6
 WIDE_BUFS = 3
-IL_BUFS = 5
-CODE_BUFS = 10
-SHARE = "PE"
-AHEAD = 3
-NB1 = 2
-NB2 = 1
-LAST = 28
-BY_PASS = 1
-ORD = ["gate","up"]
-ML = 2
-GL = 2
-GFIRST = 0
-NB0 = 0
+IL_BUFS = 6
+CODE_BUFS = 9
+TURN_BUFS = 4
+GEL_BUFS = 3
 RES_BUFS = 6
+NA = [1,2,0,0]
+SA = [3,1,1,0,4]
+NB1 = [2,3,0,3,2,1]
+NB2 = [0,1,0,0,0,0]
+SC = [3,8,1,3,3,2]
+SD = [2,2,5,3,0,2]
+OL = 0
+LAST = 26
+LAST_S = 24
+BY_PASS = 1
+ORD = ["up","gate"]
+ML = 2
+M2 = 1
+GL = 1
 SH0 = 3
-VW = 9
+SH1 = 9
+PE_AHEAD = 3
+WO_FULL = 1
+LOADS = [["wo",0,0],["at",0,0],["wo",0,1],["wo",1,2],["x",0,0],["up",0,0],["at",1,0],["x",1,0],["gate",0,0],["up",1,0],["gate",1,0],["up",0,1],["up",1,1],["gate",1,1],["gate",0,1]]
 
 F32 = mybir.dt.float32
 BF16 = mybir.dt.bfloat16
@@ -70,8 +78,14 @@ def tile_block_pb_kernel(tc, attn, x, w_out, scale2, w_gate, w_up_bytes, w_up_sc
         up_raw = {}
 
         def load_wo(g, n):
-            wo_raw[g, n] = load.tile([P, 4, SUB], BF16, name="wo_raw", bufs=4)
-            nc.sync.dma_start(out=wo_raw[g, n][:], in_=wo_v[g][:, :, n * SUB:(n + 1) * SUB])
+            if n == 2:
+                t = load.tile([P, 4, 2 * SUB], BF16, name="wo_full", bufs=WO_FULL)
+                nc.sync.dma_start(out=t[:], in_=wo_v[g])
+                wo_raw[g, 0], wo_raw[g, 1] = t[:, :, :SUB], t[:, :, SUB:]
+            else:
+                t = load.tile([P, 4, SUB], BF16, name="wo_raw", bufs=2 * (2 - WO_FULL))
+                nc.sync.dma_start(out=t[:], in_=wo_v[g][:, :, n * SUB:(n + 1) * SUB])
+                wo_raw[g, n] = t[:]
 
         def load_at(i):
             at_raw[i] = load.tile([P, 2, HD], BF16, name="at_raw", bufs=2)
@@ -89,22 +103,18 @@ def tile_block_pb_kernel(tc, attn, x, w_out, scale2, w_gate, w_up_bytes, w_up_sc
             up_raw[g, c] = load.tile([P, 4, 2 * SUB], U8, name="up_raw", bufs=UP_BUFS)
             nc.sync.dma_start(out=up_raw[g, c][:], in_=up_v[g][:, :, c * 2 * SUB:(c + 1) * 2 * SUB])
 
-        load_wo(0, 0)
-        load_up(0, 0)
-        load_wo(0, 1)
-        load_at(0)
-        load_wo(1, 0)
-        load_at(1)
-        load_wo(1, 1)
-        load_gate(0, 0)
-        load_x(0)
-        load_up(1, 0)
-        load_x(1)
-        load_gate(1, 0)
-        load_up(0, 1)
-        load_up(1, 1)
-        load_gate(0, 1)
-        load_gate(1, 1)
+        for item in LOADS:
+            kind, g, c = item
+            if kind == "wo":
+                load_wo(g, c)
+            elif kind == "at":
+                load_at(g)
+            elif kind == "x":
+                load_x(g)
+            elif kind == "gate":
+                load_gate(g, c)
+            else:
+                load_up(g, c)
 
         dummy = keep.tile([P, 1], F32)
         nc.vector.memset(dummy[:], 0.0)
@@ -143,58 +153,52 @@ def tile_block_pb_kernel(tc, attn, x, w_out, scale2, w_gate, w_up_bytes, w_up_sc
         def source(u):
             kind, c, g = u
             if kind == "wo":
-                return wo_raw[g, c][:]
+                return wo_raw[g, c]
             if kind == "gate":
                 return gate_raw[g, c // 2][:, :, (c % 2) * SUB:(c % 2 + 1) * SUB]
             return wide[u][:]
 
-        def vwiden(u):
-            return u[0] == "up" and u[2] == 1 and u[1] % VW == VW - 1
-
-        def widen(u):
+        def widen(u, t):
             kind, c, g = u
-            wide[u] = work.tile([P, 4, SUB], BF16, name="wide", bufs=WIDE_BUFS)
+            if t == 0:
+                wide[u] = work.tile([P, 4, SUB], BF16, name="wide", bufs=WIDE_BUFS)
             half = slice((c % 2) * SUB, (c % 2 + 1) * SUB)
-            for t in range(4):
-                if vwiden(u):
-                    nc.vector.tensor_scalar(
-                        out=wide[u][:, t, :],
-                        in0=up_raw[g, c // 2][:, t, half].bitcast(FP8),
-                        scalar1=upscale[:, g, t:t + 1],
-                        scalar2=None,
-                        op0=ALU.mult,
-                    )
-                    continue
-                nc.scalar.activation(
-                    out=wide[u][:, t, :],
-                    in_=up_raw[g, c // 2][:, t, half].bitcast(FP8),
-                    func=ACT.Copy,
-                    scale=upscale[:, g, t:t + 1],
-                )
+            nc.scalar.activation(
+                out=wide[u][:, t, :],
+                in_=up_raw[g, c // 2][:, t, half].bitcast(FP8),
+                func=ACT.Copy,
+                scale=upscale[:, g, t:t + 1],
+            )
 
-        def il(u, engine):
-            src = source(u)
+        def il(u):
             dst = work.tile([P, 4 * SUB], BF16, name="il", bufs=IL_BUFS, align_bytes=64)
             grouped[u] = dst
-            if engine == "PE":
-                for b in range(2):
-                    bank = psum.tile([P, 2 * SUB], BF16, name="bank")
-                    for q in range(2):
-                        c0 = (2 * b + q) * P
-                        nc.tensor.matmul(
-                            bank[:, q * SUB:(q + 1) * SUB],
-                            lhsT=ident_bf[:],
-                            rhs=src[:, :, c0:c0 + P].rearrange("p t c -> p c t"),
-                            start=True,
-                            stop=True,
-                        )
-                    nc.scalar.copy(out=dst[:, b * 2 * SUB:(b + 1) * 2 * SUB], in_=bank[:])
-            else:
-                copy = nc.vector.tensor_copy if engine == "V" else nc.scalar.copy
-                copy(
-                    out=dst[:].rearrange("p (c i t) -> p c t i", i=4, t=4),
-                    in_=src.rearrange("p t (c i) -> p c t i", i=4),
+            nc.vector.tensor_copy(
+                out=dst[:].rearrange("p (c i t) -> p c t i", i=4, t=4),
+                in_=source(u).rearrange("p t (c i) -> p c t i", i=4),
+            )
+
+        def pe_half(u, b):
+            src = source(u)
+            if b == 0:
+                grouped[u] = work.tile([P, 4 * SUB], BF16, name="il", bufs=IL_BUFS, align_bytes=64)
+            bank = psum.tile([P, 2 * SUB], BF16, name="bank")
+            banks[u, b] = bank
+            for q in range(2):
+                c0 = (2 * b + q) * P
+                nc.tensor.matmul(
+                    bank[:, q * SUB:(q + 1) * SUB].rearrange("p (c i t) -> p c t i", i=8, t=4),
+                    lhsT=ident_bf[:],
+                    rhs=src[:, :, c0:c0 + P].rearrange("p t (c i) -> p c t i", i=8),
+                    start=True,
+                    stop=True,
                 )
+
+        def copy_half(u, b):
+            nc.scalar.copy(out=grouped[u][:, b * 2 * SUB:(b + 1) * 2 * SUB], in_=banks.pop((u, b))[:])
+
+        banks = {}
+        tasks = []
 
         def quant():
             u = units[state["q"]]
@@ -208,30 +212,48 @@ def tile_block_pb_kernel(tc, attn, x, w_out, scale2, w_gate, w_up_bytes, w_up_sc
             cd, sc = codes[kind, c]
             nc.vector.quantize_mx(out=cd[:, g, :].bitcast(FP8X4), scales=sc[:, g, :], in_=grouped.pop(u)[:])
 
-        def engine_of(u):
+        def on_pe(u):
             kind, c, g = u
-            return SHARE if kind == "gate" and (g == 1 or c % SH0 == SH0 - 1) else "V"
+            return kind == "gate" and ((g == 1 and c % SH1 != SH1 - 1) or (g == 0 and c % SH0 == SH0 - 1))
 
-        def s_ahead(to):
-            while state["ahead"] < min(to, len(units)):
-                u = units[state["ahead"]]
-                state["ahead"] += 1
-                if u[0] == "up" and not vwiden(u):
-                    widen(u)
-                if engine_of(u) != "V":
-                    il(u, engine_of(u))
+        for u in units:
+            if u[0] == "up":
+                tasks += [(u, t) for t in range(4)]
+            elif on_pe(u):
+                tasks += [(u, b) for b in range(2)]
+        state["pe"] = 0
 
-        def prep(ahead=None):
+        def pe_to(n):
+            while state["pe"] < min(n, len(tasks)):
+                u, part = tasks[state["pe"]]
+                state["pe"] += 1
+                if on_pe(u):
+                    pe_half(u, part)
+
+        def s_tasks(n):
+            for _ in range(n):
+                if state["ahead"] < len(tasks):
+                    pe_to(state["ahead"] + 1 + PE_AHEAD)
+                    u, part = tasks[state["ahead"]]
+                    state["ahead"] += 1
+                    if on_pe(u):
+                        copy_half(u, part)
+                    else:
+                        widen(u, part)
+
+        def tasks_before(i):
+            ahead = units[:max(0, min(i, len(units)))]
+            return sum(4 if u[0] == "up" else 2 if on_pe(u) else 0 for u in ahead)
+
+        def prep():
             i = state["il"]
             if i in (4 + 8 - 2, 4 + 16 - 2):
                 load_more()
-            s_ahead(i + 1 + (AHEAD if ahead is None else ahead))
             if i < len(units):
+                s_tasks(tasks_before(i + 1) - state["ahead"])
                 state["il"] += 1
-                if vwiden(units[i]):
-                    widen(units[i])
-                if engine_of(units[i]) == "V":
-                    il(units[i], "V")
+                if not on_pe(units[i]):
+                    il(units[i])
             if state["q"] < state["il"] - (1 if i < len(units) else 0):
                 quant()
 
@@ -252,7 +274,7 @@ def tile_block_pb_kernel(tc, attn, x, w_out, scale2, w_gate, w_up_bytes, w_up_sc
             return bank
 
         def turn_copy(bank):
-            t = work.tile([P, G * P * 4], BF16, name="turned", bufs=2, align_bytes=64)
+            t = work.tile([P, G * P * 4], BF16, name="turned", bufs=TURN_BUFS, align_bytes=64)
             nc.scalar.copy(
                 out=t[:].bitcast(F32).rearrange("p (g r u) -> p g r u", g=G, u=2),
                 in_=bank[:].rearrange("p g u r -> p g r u"),
@@ -282,17 +304,18 @@ def tile_block_pb_kernel(tc, attn, x, w_out, scale2, w_gate, w_up_bytes, w_up_sc
         hn_q = (hn_codes, hn_scales)
 
         turned = {}
-        prep(0)
-        s_ahead(6)
         prep()
+        s_tasks(SA[0])
         prep()
         for m in range(M_TILES):
             turned[m] = turn_copy(turn_pe(at_raw[m // 2][:, m % 2, :].bitcast(F32)))
-            if m == 1:
+            s_tasks(SA[m + 1])
+            for n in range(NA[m]):
                 prep()
             if m > 0:
                 turn_quant(turned.pop(m - 1), at_q, m - 1)
-        prep()
+        for n in range(5 - 2 - sum(NA)):
+            prep()
         turn_quant(turned.pop(3), at_q, 3)
         s2b = keep.tile([P, E], BF16)
         for n in range(2):
@@ -349,7 +372,7 @@ def tile_block_pb_kernel(tc, attn, x, w_out, scale2, w_gate, w_up_bytes, w_up_sc
             mm(ub[j], hn_q, m, codes["up", c])
 
         def out_gelu(j):
-            gel[j] = work.tile([P, SUB], F32, name="gel", bufs=GL + 2)
+            gel[j] = work.tile([P, SUB], F32, name="gel", bufs=GEL_BUFS)
             nc.scalar.activation(out=gel[j][:], in_=gb.pop(j)[:], func=ACT.Gelu_apprx_tanh)
 
         def out_mul(j):
@@ -358,45 +381,65 @@ def tile_block_pb_kernel(tc, attn, x, w_out, scale2, w_gate, w_up_bytes, w_up_sc
             nc.vector.tensor_tensor(out=res[:], in0=ub.pop(j)[:], in1=gel.pop(j)[:], op=ALU.mult)
             nc.sync.dma_start(out=act_v[m][:, c * SUB:(c + 1) * SUB], in_=res[:])
 
+        steps = CHUNKS * M_TILES
+        nxt = {"mm": 0, "gelu": 0, "mul": 0}
+
+        def mm_to(n):
+            while nxt["mm"] < min(n, steps):
+                out_mm(nxt["mm"])
+                nxt["mm"] += 1
+
+        def gelu_to(n):
+            mm_to(n)
+            while nxt["gelu"] < min(n, steps):
+                out_gelu(nxt["gelu"])
+                nxt["gelu"] += 1
+
+        def mul_to(n):
+            gelu_to(n)
+            while nxt["mul"] < min(n, steps):
+                out_mul(nxt["mul"])
+                nxt["mul"] += 1
+
         h_mm(0)
         h_mm(1)
         for i in range(M_TILES + 2):
             if i < M_TILES:
                 h_add(i)
                 h_stat(i)
-            for n in range(NB1 + (i == 0) * NB0):
+            s_tasks(SC[i])
+            for n in range(NB1[i]):
                 prep()
             if 1 <= i <= M_TILES:
                 hn = h_norm(i - 1)
                 bank = turn_pe(hn[:].bitcast(F32))
+            s_tasks(SD[i])
+            if 1 <= i <= M_TILES:
                 turned[i - 1] = turn_copy(bank)
             if i + 2 < M_TILES:
                 h_mm(i + 2)
-            for n in range(NB2):
+            gelu_to(i - 2 - OL)
+            for n in range(NB2[i]):
                 prep()
             if 2 <= i:
                 turn_quant(turned.pop(i - 2), hn_q, i - 2)
+                mm_to(i - 1 - OL)
+            mul_to(i - 3 - OL)
 
-        steps = CHUNKS * M_TILES
         first = state["il"]
-        for j in range(ML):
-            out_mm(j)
-        for j in range(GL):
-            out_gelu(j)
-        for j in range(steps):
-            if GFIRST:
-                if j + ML < steps:
-                    out_mm(j + ML)
-                if j + GL < steps:
-                    out_gelu(j + GL)
-            want = first + ((j + 1) * (len(units) - first) + LAST - 1) // LAST
+        t_first = state["ahead"]
+        j0 = nxt["mul"]
+        for j in range(j0, steps):
+            mm_to(j + ML)
+            t_want = t_first + ((j + 1 - j0) * (len(tasks) - t_first)) // (LAST_S - j0)
+            n = max(0, t_want - state["ahead"])
+            s_tasks(n // 2)
+            gelu_to(j + GL)
+            s_tasks(n - n // 2)
+            want = first + ((j + 1 - j0) * (len(units) - first) + LAST - j0 - 1) // (LAST - j0)
             while state["il"] < min(want, len(units)):
                 prep()
             if state["il"] == len(units) and state["q"] < len(units):
                 prep()
-            if not GFIRST:
-                if j + ML < steps:
-                    out_mm(j + ML)
-                if j + GL < steps:
-                    out_gelu(j + GL)
-            out_mul(j)
+            mm_to(j + ML + M2)
+            mul_to(j + 1)

@@ -11,37 +11,44 @@ P = 128
 G = 2
 M_TILES = TOK // P
 SUB = 512
-CHUNKS = F // SUB
+LW = 1024
 
 FLOPS = 2 * TOK * HD * E + 2 * 2 * TOK * E * F
 
-GATE_BUFS = 5
-UP_BUFS = 6
-WIDE_BUFS = 3
-IL_BUFS = 6
+WIDTHS = [512,512,512,512,512,512,512,512]
+GATE_BUFS = 7
+UP_BUFS = 5
+TOK_BUFS = 6
+WIDE_BUFS = 4
+IL_BUFS = 5
 CODE_BUFS = 9
-TURN_BUFS = 4
-GEL_BUFS = 3
-RES_BUFS = 6
-NA = [1,2,0,0]
-SA = [3,1,1,0,4]
-NB1 = [2,3,0,3,2,1]
-NB2 = [0,1,0,0,0,0]
-SC = [3,8,1,3,3,2]
-SD = [2,2,5,3,0,2]
-OL = 0
-LAST = 26
-LAST_S = 24
-BY_PASS = 1
+TURN_BUFS = 3
+GEL_BUFS = 5
+F4K_BUFS = 6
+S0 = 2
+NA = [0,2,3,0]
+SA = [0,4,2,1,6]
+NB1 = [0,2,2,0,0,4]
+NB2 = [0,0,0,2,3,0]
+SC = [1,1,1,1,6,3]
+SD = [4,4,3,4,1,4]
+OL = 1
+LAST = 24.5
+LAST_S = 22.5
+BY_PASS = 0
 ORD = ["up","gate"]
-ML = 2
-M2 = 1
-GL = 1
-SH0 = 3
-SH1 = 9
-PE_AHEAD = 3
-WO_FULL = 1
-LOADS = [["wo",0,0],["at",0,0],["wo",0,1],["wo",1,2],["x",0,0],["up",0,0],["at",1,0],["x",1,0],["gate",0,0],["up",1,0],["gate",1,0],["up",0,1],["up",1,1],["gate",1,1],["gate",0,1]]
+ML = 1
+M2 = 0
+GL = 3
+PE1 = 7
+PE0 = 7
+SI1 = 3
+SI0 = 2
+PE_AHEAD = 4
+PE_AHEAD_B = 2
+LOAD_LEAD = 512
+LOADS = [["up0",0,0],["up1",0,0],["wo",1,2],["wo",0,2],["at",0,0],["at",2,0],["gate",0,0],["at",1,0],["up0",1,0],["up1",1,0],["at",3,0],["x",0,0],["x",1,0],["gate",1,0],["gate",0,1],["up",0,1],["x",3,0],["up",1,1],["x",2,0],["gate",1,1]]
+HEAD = [["up",0,0],["wo",1,1],["wo",1,0],["wo",0,0],["wo",0,1],["gate",0,0],["up",1,0]]
 
 F32 = mybir.dt.float32
 BF16 = mybir.dt.bfloat16
@@ -79,42 +86,35 @@ def tile_block_pb_kernel(tc, attn, x, w_out, scale2, w_gate, w_up_bytes, w_up_sc
 
         def load_wo(g, n):
             if n == 2:
-                t = load.tile([P, 4, 2 * SUB], BF16, name="wo_full", bufs=WO_FULL)
+                t = load.tile([P, 4, LW], BF16, name="gate_raw", bufs=GATE_BUFS)
                 nc.sync.dma_start(out=t[:], in_=wo_v[g])
-                wo_raw[g, 0], wo_raw[g, 1] = t[:, :, :SUB], t[:, :, SUB:]
+                wo_raw[g] = [t[:, :, :SUB], t[:, :, SUB:]]
             else:
-                t = load.tile([P, 4, SUB], BF16, name="wo_raw", bufs=2 * (2 - WO_FULL))
-                nc.sync.dma_start(out=t[:], in_=wo_v[g][:, :, n * SUB:(n + 1) * SUB])
-                wo_raw[g, n] = t[:]
+                if g not in wo_raw:
+                    t = load.tile([P, 2, 4, SUB], BF16, name="gate_raw", bufs=GATE_BUFS)
+                    wo_raw[g] = [t[:, 0], t[:, 1]]
+                nc.sync.dma_start(out=wo_raw[g][n], in_=wo_v[g][:, :, n * SUB:(n + 1) * SUB])
 
         def load_at(i):
-            at_raw[i] = load.tile([P, 2, HD], BF16, name="at_raw", bufs=2)
-            nc.sync.dma_start(out=at_raw[i][:], in_=attn_v[:, 2 * i:2 * i + 2, :])
+            at_raw[i] = load.tile([P, HD], BF16, name="tok", bufs=TOK_BUFS)
+            nc.sync.dma_start(out=at_raw[i][:], in_=attn_v[:, i, :])
 
         def load_x(i):
-            x_raw[i] = load.tile([P, 2, E], BF16, name="x_raw", bufs=2)
-            nc.sync.dma_start(out=x_raw[i][:], in_=x_v[:, 2 * i:2 * i + 2, :])
+            x_raw[i] = load.tile([P, E], BF16, name="tok", bufs=TOK_BUFS)
+            nc.sync.dma_start(out=x_raw[i][:], in_=x_v[:, i, :])
 
         def load_gate(g, c):
-            gate_raw[g, c] = load.tile([P, 4, 2 * SUB], BF16, name="gate_raw", bufs=GATE_BUFS)
-            nc.sync.dma_start(out=gate_raw[g, c][:], in_=gate_v[g][:, :, c * 2 * SUB:(c + 1) * 2 * SUB])
+            gate_raw[g, c] = load.tile([P, 4, LW], BF16, name="gate_raw", bufs=GATE_BUFS)
+            nc.sync.dma_start(out=gate_raw[g, c][:], in_=gate_v[g][:, :, c * LW:(c + 1) * LW])
 
-        def load_up(g, c):
-            up_raw[g, c] = load.tile([P, 4, 2 * SUB], U8, name="up_raw", bufs=UP_BUFS)
-            nc.sync.dma_start(out=up_raw[g, c][:], in_=up_v[g][:, :, c * 2 * SUB:(c + 1) * 2 * SUB])
+        def load_up(g, c, t0=0, t1=4):
+            if (g, c) not in up_raw:
+                up_raw[g, c] = load.tile([P, 4, LW], U8, name="up_raw", bufs=UP_BUFS)
+            nc.sync.dma_start(out=up_raw[g, c][:, t0:t1, :], in_=up_v[g][:, t0:t1, c * LW:(c + 1) * LW])
 
-        for item in LOADS:
-            kind, g, c = item
-            if kind == "wo":
-                load_wo(g, c)
-            elif kind == "at":
-                load_at(g)
-            elif kind == "x":
-                load_x(g)
-            elif kind == "gate":
-                load_gate(g, c)
-            else:
-                load_up(g, c)
+        for kind, g, c in LOADS:
+            {"wo": lambda: load_wo(g, c), "at": lambda: load_at(g), "x": lambda: load_x(g),
+             "gate": lambda: load_gate(g, c), "up": lambda: load_up(g, c), "up0": lambda: load_up(g, c, 0, 2), "up1": lambda: load_up(g, c, 2, 4)}[kind]()
 
         dummy = keep.tile([P, 1], F32)
         nc.vector.memset(dummy[:], 0.0)
@@ -124,7 +124,7 @@ def tile_block_pb_kernel(tc, attn, x, w_out, scale2, w_gate, w_up_bytes, w_up_sc
         nc.scalar.dma_start(out=upscale[:], in_=upscale_v)
         ident = keep.tile([P, P], F32)
         make_identity(nc, ident[:])
-        s2row = keep.tile([P, E], BF16)
+        s2row = work.tile([P, E], BF16, name="hn", bufs=2)
         nc.gpsimd.memset(s2row[:].bitcast(F32), 0.0)
         nc.gpsimd.dma_start(out=s2row[0:1, :], in_=scale2.rearrange("(o e) -> o e", o=1))
         ones = keep.tile([P, P], BF16)
@@ -134,137 +134,194 @@ def tile_block_pb_kernel(tc, attn, x, w_out, scale2, w_gate, w_up_bytes, w_up_sc
         neghalf = keep.tile([P, 1], F32)
         nc.gpsimd.memset(neghalf[:], -0.5)
 
+        chunks = []
+        c0 = 0
+        for w in WIDTHS:
+            chunks.append((c0, w))
+            c0 += w
         units = []
-        for g in range(G):
-            for n in range(2):
-                units.append(("wo", n, g))
-        for c in range(0, CHUNKS, 2):
-            pair = [(c, g) for g in range(G)] + [(c + 1, g) for g in range(G)]
-            if c < 2 * BY_PASS:
-                pair = [(d, g) for g in range(G) for d in (c, c + 1)]
-            for d, g in pair:
-                units.append((ORD[0], d, g))
-                units.append((ORD[1], d, g))
-        codes = {}
+        for kind, n, g in HEAD:
+            units.append((kind, (n * SUB, SUB) if kind == "wo" else chunks[n], g))
+        n_wo = max(i for i, u in enumerate(units) if u[0] == "wo") + 1
+        for lt in range(F // LW):
+            part = [ch for ch in chunks if ch[0] // LW == lt]
+            if lt < BY_PASS:
+                pairs = [(ch, g) for g in range(G) for ch in part]
+            else:
+                pairs = [(ch, g) for ch in part for g in range(G)]
+            for ch, g in pairs:
+                units += [u for u in ((ORD[0], ch, g), (ORD[1], ch, g)) if u not in units]
         grouped = {}
         wide = {}
-        state = {"ahead": 0, "il": 0, "q": 0, "load": 2}
+        banks = {}
+        codes = {}
+        state = {"task": 0, "pe": 0, "il": 0, "q": 0, "load": 2, "lead": 0}
+
+        def pe_blocks(u):
+            kind, (c, w), g = u
+            if kind != "gate":
+                return 0
+            n = PE1 if g == 1 else PE0
+            b0, b1 = c // 256, (c + w) // 256
+            return (b1 * n) // 16 - (b0 * n) // 16
+
+        def sc_blocks(u):
+            kind, (c, w), g = u
+            if kind != "gate":
+                return 0
+            n = SI1 if g == 1 else SI0
+            b0, b1 = c // 256, (c + w) // 256
+            return min((b1 * n) // 16 - (b0 * n) // 16, b1 - b0 - pe_blocks(u))
 
         def source(u):
-            kind, c, g = u
+            kind, (c, w), g = u
             if kind == "wo":
-                return wo_raw[g, c]
+                if w == LW:
+                    return None
+                return wo_raw[g][c // SUB]
             if kind == "gate":
-                return gate_raw[g, c // 2][:, :, (c % 2) * SUB:(c % 2 + 1) * SUB]
+                ensure(c // LW)
+                return gate_raw[g, c // LW][:, :, c % LW:c % LW + w]
             return wide[u][:]
 
+        def new_il(u):
+            grouped[u] = work.tile([P, 4 * u[1][1]], BF16, name="il", bufs=IL_BUFS, align_bytes=64)
+
+        def ensure(lt):
+            while state["load"] <= lt:
+                load_more()
+
         def widen(u, t):
-            kind, c, g = u
+            kind, (c, w), g = u
+            ensure(c // LW)
             if t == 0:
-                wide[u] = work.tile([P, 4, SUB], BF16, name="wide", bufs=WIDE_BUFS)
-            half = slice((c % 2) * SUB, (c % 2 + 1) * SUB)
+                wide[u] = work.tile([P, 4, w], BF16, name="wide", bufs=WIDE_BUFS)
             nc.scalar.activation(
                 out=wide[u][:, t, :],
-                in_=up_raw[g, c // 2][:, t, half].bitcast(FP8),
+                in_=up_raw[g, c // LW][:, t, c % LW:c % LW + w].bitcast(FP8),
                 func=ACT.Copy,
                 scale=upscale[:, g, t:t + 1],
             )
 
-        def il(u):
-            dst = work.tile([P, 4 * SUB], BF16, name="il", bufs=IL_BUFS, align_bytes=64)
-            grouped[u] = dst
-            nc.vector.tensor_copy(
-                out=dst[:].rearrange("p (c i t) -> p c t i", i=4, t=4),
-                in_=source(u).rearrange("p t (c i) -> p c t i", i=4),
-            )
-
-        def pe_half(u, b):
-            src = source(u)
+        def pe_block(u, b):
             if b == 0:
-                grouped[u] = work.tile([P, 4 * SUB], BF16, name="il", bufs=IL_BUFS, align_bytes=64)
+                new_il(u)
             bank = psum.tile([P, 2 * SUB], BF16, name="bank")
             banks[u, b] = bank
             for q in range(2):
                 c0 = (2 * b + q) * P
                 nc.tensor.matmul(
-                    bank[:, q * SUB:(q + 1) * SUB].rearrange("p (c i t) -> p c t i", i=8, t=4),
+                    bank[:, q * SUB:(q + 1) * SUB].rearrange("p (i t) -> p t i", t=4),
                     lhsT=ident_bf[:],
-                    rhs=src[:, :, c0:c0 + P].rearrange("p t (c i) -> p c t i", i=8),
+                    rhs=source(u)[:, :, c0:c0 + P],
                     start=True,
                     stop=True,
                 )
 
-        def copy_half(u, b):
+        def copy_block(u, b):
+            if b >= pe_blocks(u):
+                if b == 0:
+                    new_il(u)
+                nc.scalar.copy(
+                    out=grouped[u][:, b * 2 * SUB:(b + 1) * 2 * SUB].rearrange("p (c i t) -> p c t i", i=4, t=4),
+                    in_=source(u)[:, :, b * 256:(b + 1) * 256].rearrange("p t (c i) -> p c t i", i=4),
+                )
+                return
             nc.scalar.copy(out=grouped[u][:, b * 2 * SUB:(b + 1) * 2 * SUB], in_=banks.pop((u, b))[:])
 
-        banks = {}
         tasks = []
-
-        def quant():
-            u = units[state["q"]]
-            state["q"] += 1
-            kind, c, g = u
-            if g == 0:
-                codes[kind, c] = (
-                    work.tile([P, G, SUB], U32, name="codes", bufs=CODE_BUFS, align_bytes=64),
-                    work.tile([P, G, SUB], U8, name="scales", bufs=CODE_BUFS, align_bytes=64),
-                )
-            cd, sc = codes[kind, c]
-            nc.vector.quantize_mx(out=cd[:, g, :].bitcast(FP8X4), scales=sc[:, g, :], in_=grouped.pop(u)[:])
-
-        def on_pe(u):
-            kind, c, g = u
-            return kind == "gate" and ((g == 1 and c % SH1 != SH1 - 1) or (g == 0 and c % SH0 == SH0 - 1))
-
         for u in units:
             if u[0] == "up":
-                tasks += [(u, t) for t in range(4)]
-            elif on_pe(u):
-                tasks += [(u, b) for b in range(2)]
-        state["pe"] = 0
+                tasks += [(u, t, u[1][1]) for t in range(4)]
+            tasks += [(u, b, 512 if b < pe_blocks(u) else 1060) for b in range(pe_blocks(u) + sc_blocks(u))]
 
         def pe_to(n):
             while state["pe"] < min(n, len(tasks)):
-                u, part = tasks[state["pe"]]
+                u, part, cost = tasks[state["pe"]]
                 state["pe"] += 1
-                if on_pe(u):
-                    pe_half(u, part)
+                if u[0] == "gate" and part < pe_blocks(u):
+                    pe_block(u, part)
 
         def s_tasks(n):
             for _ in range(n):
-                if state["ahead"] < len(tasks):
-                    pe_to(state["ahead"] + 1 + PE_AHEAD)
-                    u, part = tasks[state["ahead"]]
-                    state["ahead"] += 1
-                    if on_pe(u):
-                        copy_half(u, part)
+                if state["task"] < len(tasks):
+                    pe_to(state["task"] + 1 + state["lead"])
+                    u, part, cost = tasks[state["task"]]
+                    state["task"] += 1
+                    if u[0] == "gate":
+                        copy_block(u, part)
                     else:
                         widen(u, part)
 
         def tasks_before(i):
-            ahead = units[:max(0, min(i, len(units)))]
-            return sum(4 if u[0] == "up" else 2 if on_pe(u) else 0 for u in ahead)
+            return sum(1 for t in tasks if t[0] in units[:i])
 
-        def prep():
-            i = state["il"]
-            if i in (4 + 8 - 2, 4 + 16 - 2):
-                load_more()
-            if i < len(units):
-                s_tasks(tasks_before(i + 1) - state["ahead"])
-                state["il"] += 1
-                if not on_pe(units[i]):
-                    il(units[i])
-            if state["q"] < state["il"] - (1 if i < len(units) else 0):
-                quant()
+        def il(u):
+            kind, (c, w), g = u
+            pe = 256 * (pe_blocks(u) + sc_blocks(u))
+            if pe == 0:
+                new_il(u)
+            if kind == "wo" and w == LW:
+                for n in range(2):
+                    nc.vector.tensor_copy(
+                        out=grouped[u][:, n * 4 * SUB:(n + 1) * 4 * SUB].rearrange("p (c i t) -> p c t i", i=4, t=4),
+                        in_=wo_raw[g][n].rearrange("p t (c i) -> p c t i", i=4),
+                    )
+            elif pe < w:
+                nc.vector.tensor_copy(
+                    out=grouped[u][:, 4 * pe:].rearrange("p (c i t) -> p c t i", i=4, t=4),
+                    in_=source(u)[:, :, pe:].rearrange("p t (c i) -> p c t i", i=4),
+                )
+
+        def quant():
+            u = units[state["q"]]
+            state["q"] += 1
+            kind, (c, w), g = u
+            if kind == "wo":
+                if "wo" not in codes:
+                    codes["wo"] = (
+                        keep.tile([P, G, LW], U32, name="wo_codes", align_bytes=64),
+                        keep.tile([P, G, LW], U8, name="wo_scales", align_bytes=64),
+                    )
+                cd, sc = codes["wo"]
+                cols = slice(c, c + w)
+            else:
+                if (kind, c) not in codes:
+                    codes[kind, c] = (
+                        work.tile([P, G, w], U32, name="codes", bufs=CODE_BUFS, align_bytes=64),
+                        work.tile([P, G, w], U8, name="scales", bufs=CODE_BUFS, align_bytes=64),
+                    )
+                cd, sc = codes[kind, c]
+                cols = slice(0, w)
+            nc.vector.quantize_mx(out=cd[:, g, cols].bitcast(FP8X4), scales=sc[:, g, cols], in_=grouped.pop(u)[:])
 
         def load_more():
             c = state["load"]
-            if c < 4:
+            if c < F // LW:
                 state["load"] += 1
                 load_gate(0, c)
                 load_up(0, c)
                 load_gate(1, c)
                 load_up(1, c)
+
+        def prep():
+            i = state["il"]
+            if i < len(units):
+                kind, (c, w), g = units[i]
+                need = 1 if i < len(HEAD) else min(F // LW - 1, c // LW + 1 + (c % LW + w > LW - LOAD_LEAD))
+                while state["load"] <= need:
+                    load_more()
+                s_tasks(tasks_before(i + 1) - state["task"])
+                state["il"] += 1
+                il(units[i])
+            if state["q"] < state["il"] - (1 if i < len(units) else 0):
+                quant()
+
+        def v_cols():
+            return sum(u[1][1] for u in units[:state["il"]])
+
+        def s_cost():
+            return sum(t[2] for t in tasks[:state["task"]])
 
         def turn_pe(words):
             bank = psum.tile([P, G, 2, P], F32, name="bank")
@@ -284,14 +341,14 @@ def tile_block_pb_kernel(tc, attn, x, w_out, scale2, w_gate, w_up_bytes, w_up_sc
         def turn_quant(t, dst, m):
             nc.vector.quantize_mx(out=dst[0][:, m, :].bitcast(FP8X4), scales=dst[1][:, m, :], in_=t[:])
 
-        def mm(bank, lhs, m, rhs):
+        def mm(bank, lhs, m, rhs, c, w):
             for g in range(G):
                 nc.tensor.matmul_mx(
                     out=bank[:],
                     lhsT=lhs[0][:, m, g * P:(g + 1) * P].bitcast(FP8X4),
                     lhsT_scale=lhs[1][:, m, g * P:(g + 1) * P],
-                    rhs=rhs[0][:, g, :].bitcast(FP8X4),
-                    rhs_scale=rhs[1][:, g, :],
+                    rhs=rhs[0][:, g, c:c + w].bitcast(FP8X4),
+                    rhs_scale=rhs[1][:, g, c:c + w],
                     start=(g == 0),
                     stop=(g == G - 1),
                 )
@@ -304,24 +361,24 @@ def tile_block_pb_kernel(tc, attn, x, w_out, scale2, w_gate, w_up_bytes, w_up_sc
         hn_q = (hn_codes, hn_scales)
 
         turned = {}
+        s_tasks(S0)
         prep()
         s_tasks(SA[0])
         prep()
         for m in range(M_TILES):
-            turned[m] = turn_copy(turn_pe(at_raw[m // 2][:, m % 2, :].bitcast(F32)))
+            turned[m] = turn_copy(turn_pe(at_raw[m][:].bitcast(F32)))
             s_tasks(SA[m + 1])
             for n in range(NA[m]):
                 prep()
             if m > 0:
                 turn_quant(turned.pop(m - 1), at_q, m - 1)
-        for n in range(5 - 2 - sum(NA)):
+        while state["q"] < n_wo:
             prep()
         turn_quant(turned.pop(3), at_q, 3)
-        s2b = keep.tile([P, E], BF16)
+        s2b = psum.tile([P, E], BF16, name="bank")
         for n in range(2):
-            bank = psum.tile([P, SUB], F32, name="bank")
-            nc.tensor.matmul(bank[:], lhsT=ones[:], rhs=s2row[:, n * SUB:(n + 1) * SUB], start=True, stop=True)
-            nc.scalar.copy(out=s2b[:, n * SUB:(n + 1) * SUB], in_=bank[:])
+            cols = slice(n * SUB, (n + 1) * SUB)
+            nc.tensor.matmul(s2b[:, cols], lhsT=ones[:], rhs=s2row[:, cols], start=True, stop=True)
 
         h_banks = {}
         h_t = {}
@@ -330,19 +387,19 @@ def tile_block_pb_kernel(tc, attn, x, w_out, scale2, w_gate, w_up_bytes, w_up_sc
         def h_mm(m):
             for n in range(2):
                 h_banks[m, n] = psum.tile([P, SUB], F32, name="bank")
-                mm(h_banks[m, n], at_q, m, codes["wo", n])
+                mm(h_banks[m, n], at_q, m, codes["wo"], n * SUB, SUB)
 
         def h_add(m):
-            h_t[m] = work.tile([P, E], F32, name="h", bufs=2)
+            h_t[m] = work.tile([P, E], F32, name="f4k", bufs=F4K_BUFS)
             for n in range(2):
                 cols = slice(n * SUB, (n + 1) * SUB)
                 nc.vector.tensor_tensor(
-                    out=h_t[m][:, cols], in0=h_banks.pop((m, n))[:], in1=x_raw[m // 2][:, m % 2, cols], op=ALU.add
+                    out=h_t[m][:, cols], in0=h_banks.pop((m, n))[:], in1=x_raw[m][:, cols], op=ALU.add
                 )
             nc.sync.dma_start(out=h_v[m], in_=h_t[m][:])
 
         def h_stat(m):
-            junk = work.tile([P, E], F32, name="junk", bufs=1)
+            junk = work.tile([P, E], F32, name="f4k", bufs=F4K_BUFS)
             stat = work.tile([P, 8], F32, name="stat", bufs=2)
             var = work.tile([P, 8], F32, name="var", bufs=2)
             r_t[m] = work.tile([P, 8], F32, name="rstd", bufs=2)
@@ -357,50 +414,56 @@ def tile_block_pb_kernel(tc, attn, x, w_out, scale2, w_gate, w_up_bytes, w_up_sc
             )
             return hn
 
+        steps = [
+            (ch, m, p0, min(SUB, ch[1])) for ch in chunks for m in range(M_TILES) for p0 in range(0, ch[1], SUB)
+        ]
         gb = {}
         ub = {}
         gel = {}
+        res = {}
+        nxt = {"mm": 0, "gelu": 0, "mul": 0}
 
         def out_mm(j):
-            c, m = divmod(j, M_TILES)
-            last = max(units.index(("gate", c, 1)), units.index(("up", c, 1)))
+            (c, w), m, p0, pw = steps[j]
+            last = max(units.index(("gate", (c, w), 1)), units.index(("up", (c, w), 1)))
             while state["q"] <= last:
                 prep()
-            gb[j] = psum.tile([P, SUB], F32, name="bank")
-            mm(gb[j], hn_q, m, codes["gate", c])
-            ub[j] = psum.tile([P, SUB], F32, name="bank")
-            mm(ub[j], hn_q, m, codes["up", c])
+            gb[j] = psum.tile([P, pw], F32, name="bank")
+            mm(gb[j], hn_q, m, codes["gate", c], p0, pw)
+            ub[j] = psum.tile([P, pw], F32, name="bank")
+            mm(ub[j], hn_q, m, codes["up", c], p0, pw)
 
         def out_gelu(j):
-            gel[j] = work.tile([P, SUB], F32, name="gel", bufs=GEL_BUFS)
+            gel[j] = work.tile([P, steps[j][3]], F32, name="gel", bufs=GEL_BUFS)
             nc.scalar.activation(out=gel[j][:], in_=gb.pop(j)[:], func=ACT.Gelu_apprx_tanh)
 
         def out_mul(j):
-            c, m = divmod(j, M_TILES)
-            res = work.tile([P, SUB], F32, name="res", bufs=RES_BUFS)
-            nc.vector.tensor_tensor(out=res[:], in0=ub.pop(j)[:], in1=gel.pop(j)[:], op=ALU.mult)
-            nc.sync.dma_start(out=act_v[m][:, c * SUB:(c + 1) * SUB], in_=res[:])
-
-        steps = CHUNKS * M_TILES
-        nxt = {"mm": 0, "gelu": 0, "mul": 0}
+            (c, w), m, p0, pw = steps[j]
+            if p0 == 0:
+                res[m] = work.tile([P, w], F32, name="f4k", bufs=F4K_BUFS)
+            nc.vector.tensor_tensor(out=res[m][:, p0:p0 + pw], in0=ub.pop(j)[:], in1=gel.pop(j)[:], op=ALU.mult)
+            if p0 + pw == w:
+                nc.sync.dma_start(out=act_v[m][:, c:c + w], in_=res[m][:])
 
         def mm_to(n):
-            while nxt["mm"] < min(n, steps):
+            while nxt["mm"] < min(n, len(steps)):
                 out_mm(nxt["mm"])
                 nxt["mm"] += 1
 
         def gelu_to(n):
             mm_to(n)
-            while nxt["gelu"] < min(n, steps):
+            while nxt["gelu"] < min(n, len(steps)):
                 out_gelu(nxt["gelu"])
                 nxt["gelu"] += 1
 
         def mul_to(n):
             gelu_to(n)
-            while nxt["mul"] < min(n, steps):
+            while nxt["mul"] < min(n, len(steps)):
                 out_mul(nxt["mul"])
                 nxt["mul"] += 1
 
+        per_m = max(1, chunks[0][1] // SUB)
+        state["lead"] = PE_AHEAD_B
         h_mm(0)
         h_mm(1)
         for i in range(M_TILES + 2):
@@ -418,26 +481,32 @@ def tile_block_pb_kernel(tc, attn, x, w_out, scale2, w_gate, w_up_bytes, w_up_sc
                 turned[i - 1] = turn_copy(bank)
             if i + 2 < M_TILES:
                 h_mm(i + 2)
-            gelu_to(i - 2 - OL)
+            gelu_to(per_m * (i - 2 - OL))
             for n in range(NB2[i]):
                 prep()
             if 2 <= i:
                 turn_quant(turned.pop(i - 2), hn_q, i - 2)
-                mm_to(i - 1 - OL)
-            mul_to(i - 3 - OL)
+                mm_to(per_m * (i - 1 - OL))
+            mul_to(per_m * (i - 3 - OL))
 
-        first = state["il"]
-        t_first = state["ahead"]
-        j0 = nxt["mul"]
-        for j in range(j0, steps):
+        state["lead"] = PE_AHEAD
+        def cum(j):
+            return sum(s[3] for s in steps[:j])
+
+        v0, s0, k0 = v_cols(), s_cost(), cum(nxt["mul"])
+        v_all, s_all = sum(u[1][1] for u in units), sum(t[2] for t in tasks)
+        for j in range(nxt["mul"], len(steps)):
+            done = cum(j + 1) - k0
             mm_to(j + ML)
-            t_want = t_first + ((j + 1 - j0) * (len(tasks) - t_first)) // (LAST_S - j0)
-            n = max(0, t_want - state["ahead"])
-            s_tasks(n // 2)
+            n = state["task"]
+            want = s0 + (s_all - s0) * done / (LAST_S * 512 - k0)
+            while state["task"] < len(tasks) and s_cost() + tasks[state["task"]][2] / 2 < want:
+                s_tasks(1)
+                if state["task"] == n + 1:
+                    gelu_to(j + GL)
             gelu_to(j + GL)
-            s_tasks(n - n // 2)
-            want = first + ((j + 1 - j0) * (len(units) - first) + LAST - j0 - 1) // (LAST - j0)
-            while state["il"] < min(want, len(units)):
+            want = v0 + (v_all - v0) * done / (LAST * 512 - k0)
+            while state["il"] < len(units) and v_cols() + units[state["il"]][1][1] / 2 < want:
                 prep()
             if state["il"] == len(units) and state["q"] < len(units):
                 prep()

from contextlib import ExitStack

import concourse.mybir as mybir
from concourse.masks import make_identity

B, S, E, H, D, F = 2, 256, 1024, 8, 128, 4096
EPS = 1e-6
TOK = B * S
HD = H * D
P = 128
G = 2
M_TILES = TOK // P
SUB = 512
LW = 1024

FLOPS = 2 * TOK * HD * E + 2 * 2 * TOK * E * F

WIDTHS = [512,512,512,512,512,512,512,512]
GATE_BUFS = 7
UP_BUFS = 5
TOK_BUFS = 6
WIDE_BUFS = 4
IL_BUFS = 5
CODE_BUFS = 9
TURN_BUFS = 3
GEL_BUFS = 5
F4K_BUFS = 6
S0 = 2
NA = [0,2,3,0]
SA = [0,4,2,1,6]
NB1 = [0,2,2,0,0,4]
NB2 = [0,0,0,2,3,0]
SC = [1,1,1,1,6,3]
SD = [4,4,3,4,1,4]
OL = 1
LAST = 24.5
LAST_S = 22.5
BY_PASS = 0
ORD = ["up","gate"]
ML = 1
M2 = 0
GL = 3
PE1 = 7
PE0 = 7
SI1 = 3
SI0 = 2
PE_AHEAD = 4
PE_AHEAD_B = 2
LOAD_LEAD = 512
LOADS = [["up0",0,0],["up1",0,0],["wo",1,2],["wo",0,2],["at",0,0],["at",2,0],["gate",0,0],["at",1,0],["up0",1,0],["up1",1,0],["at",3,0],["x",0,0],["x",1,0],["gate",1,0],["gate",0,1],["up",0,1],["x",3,0],["up",1,1],["x",2,0],["gate",1,1]]
HEAD = [["up",0,0],["wo",1,1],["wo",1,0],["wo",0,0],["wo",0,1],["gate",0,0],["up",1,0]]

F32 = mybir.dt.float32
BF16 = mybir.dt.bfloat16
U32 = mybir.dt.uint32
U8 = mybir.dt.uint8
FP8 = mybir.dt.float8_e4m3fn
FP8X4 = mybir.dt.float8_e4m3fn_x4
ALU = mybir.AluOpType
ACT = mybir.ActivationFunctionType


def tile_block_pb_kernel(tc, attn, x, w_out, scale2, w_gate, w_up_bytes, w_up_scale, h_out, act_out):
    nc = tc.nc
    attn_v = attn.rearrange("b s h d -> (b s) (h d)").rearrange("(m p) k -> p m k", p=P)
    x_v = x.rearrange("b s e -> (b s) e").rearrange("(m p) e -> p m e", p=P)
    wo_v = w_out.rearrange("h d e -> (h d) e").rearrange("(g p t) n -> g p t n", p=P, t=4)
    gate_v = w_gate.rearrange("(g p t) n -> g p t n", p=P, t=4)
    up_v = w_up_bytes.rearrange("(g p t) n -> g p t n", p=P, t=4)
    upscale_v = w_up_scale.rearrange("(g p t) o -> p g (t o)", p=P, t=4)
    h_v = h_out.rearrange("b s e -> (b s) e").rearrange("(m p) e -> m p e", p=P)
    act_v = act_out.rearrange("b s f -> (b s) f").rearrange("(m p) f -> m p f", p=P)

    with ExitStack() as ctx:
        ctx.enter_context(tc.manual_schedule())
        keep = ctx.enter_context(tc.tile_pool(name="keep", bufs=1))
        load = ctx.enter_context(tc.tile_pool(name="load", bufs=1))
        work = ctx.enter_context(tc.tile_pool(name="work", bufs=1))
        psum = ctx.enter_context(tc.psum_pool(name="psum", bufs=8))

        wo_raw = {}
        at_raw = {}
        x_raw = {}
        gate_raw = {}
        up_raw = {}

        def load_wo(g, n):
            if n == 2:
                t = load.tile([P, 4, LW], BF16, name="gate_raw", bufs=GATE_BUFS)
                nc.sync.dma_start(out=t[:], in_=wo_v[g])
                wo_raw[g] = [t[:, :, :SUB], t[:, :, SUB:]]
            else:
                if g not in wo_raw:
                    t = load.tile([P, 2, 4, SUB], BF16, name="gate_raw", bufs=GATE_BUFS)
                    wo_raw[g] = [t[:, 0], t[:, 1]]
                nc.sync.dma_start(out=wo_raw[g][n], in_=wo_v[g][:, :, n * SUB:(n + 1) * SUB])

        def load_at(i):
            at_raw[i] = load.tile([P, HD], BF16, name="tok", bufs=TOK_BUFS)
            nc.sync.dma_start(out=at_raw[i][:], in_=attn_v[:, i, :])

        def load_x(i):
            x_raw[i] = load.tile([P, E], BF16, name="tok", bufs=TOK_BUFS)
            nc.sync.dma_start(out=x_raw[i][:], in_=x_v[:, i, :])

        def load_gate(g, c):
            gate_raw[g, c] = load.tile([P, 4, LW], BF16, name="gate_raw", bufs=GATE_BUFS)
            nc.sync.dma_start(out=gate_raw[g, c][:], in_=gate_v[g][:, :, c * LW:(c + 1) * LW])

        def load_up(g, c, t0=0, t1=4):
            if (g, c) not in up_raw:
                up_raw[g, c] = load.tile([P, 4, LW], U8, name="up_raw", bufs=UP_BUFS)
            nc.sync.dma_start(out=up_raw[g, c][:, t0:t1, :], in_=up_v[g][:, t0:t1, c * LW:(c + 1) * LW])

        for kind, g, c in LOADS:
            {"wo": lambda: load_wo(g, c), "at": lambda: load_at(g), "x": lambda: load_x(g),
             "gate": lambda: load_gate(g, c), "up": lambda: load_up(g, c), "up0": lambda: load_up(g, c, 0, 2), "up1": lambda: load_up(g, c, 2, 4)}[kind]()

        dummy = keep.tile([P, 1], F32)
        nc.vector.memset(dummy[:], 0.0)
        dummy2 = keep.tile([P, 1], F32)
        nc.scalar.activation(out=dummy2[:], in_=dummy[:], func=ACT.Gelu_apprx_tanh)
        upscale = keep.tile([P, G, 4], F32)
        nc.scalar.dma_start(out=upscale[:], in_=upscale_v)
        ident = keep.tile([P, P], F32)
        make_identity(nc, ident[:])
        s2row = work.tile([P, E], BF16, name="hn", bufs=2)
        nc.gpsimd.memset(s2row[:].bitcast(F32), 0.0)
        nc.gpsimd.dma_start(out=s2row[0:1, :], in_=scale2.rearrange("(o e) -> o e", o=1))
        ones = keep.tile([P, P], BF16)
        nc.gpsimd.memset(ones[:], 1.0)
        ident_bf = keep.tile([P, P], BF16)
        nc.vector.tensor_copy(out=ident_bf[:], in_=ident[:])
        neghalf = keep.tile([P, 1], F32)
        nc.gpsimd.memset(neghalf[:], -0.5)

        chunks = []
        c0 = 0
        for w in WIDTHS:
            chunks.append((c0, w))
            c0 += w
        units = []
        for kind, n, g in HEAD:
            units.append((kind, (n * SUB, SUB) if kind == "wo" else chunks[n], g))
        n_wo = max(i for i, u in enumerate(units) if u[0] == "wo") + 1
        for lt in range(F // LW):
            part = [ch for ch in chunks if ch[0] // LW == lt]
            if lt < BY_PASS:
                pairs = [(ch, g) for g in range(G) for ch in part]
            else:
                pairs = [(ch, g) for ch in part for g in range(G)]
            for ch, g in pairs:
                units += [u for u in ((ORD[0], ch, g), (ORD[1], ch, g)) if u not in units]
        grouped = {}
        wide = {}
        banks = {}
        codes = {}
        state = {"task": 0, "pe": 0, "il": 0, "q": 0, "load": 2, "lead": 0}

        def pe_blocks(u):
            kind, (c, w), g = u
            if kind != "gate":
                return 0
            n = PE1 if g == 1 else PE0
            b0, b1 = c // 256, (c + w) // 256
            return (b1 * n) // 16 - (b0 * n) // 16

        def sc_blocks(u):
            kind, (c, w), g = u
            if kind != "gate":
                return 0
            n = SI1 if g == 1 else SI0
            b0, b1 = c // 256, (c + w) // 256
            return min((b1 * n) // 16 - (b0 * n) // 16, b1 - b0 - pe_blocks(u))

        def source(u):
            kind, (c, w), g = u
            if kind == "wo":
                if w == LW:
                    return None
                return wo_raw[g][c // SUB]
            if kind == "gate":
                ensure(c // LW)
                return gate_raw[g, c // LW][:, :, c % LW:c % LW + w]
            return wide[u][:]

        def new_il(u):
            grouped[u] = work.tile([P, 4 * u[1][1]], BF16, name="il", bufs=IL_BUFS, align_bytes=64)

        def ensure(lt):
            while state["load"] <= lt:
                load_more()

        def widen(u, t):
            kind, (c, w), g = u
            ensure(c // LW)
            if t == 0:
                wide[u] = work.tile([P, 4, w], BF16, name="wide", bufs=WIDE_BUFS)
            nc.scalar.activation(
                out=wide[u][:, t, :],
                in_=up_raw[g, c // LW][:, t, c % LW:c % LW + w].bitcast(FP8),
                func=ACT.Copy,
                scale=upscale[:, g, t:t + 1],
            )

        def pe_block(u, b):
            if b == 0:
                new_il(u)
            bank = psum.tile([P, 2 * SUB], BF16, name="bank")
            banks[u, b] = bank
            for q in range(2):
                c0 = (2 * b + q) * P
                nc.tensor.matmul(
                    bank[:, q * SUB:(q + 1) * SUB].rearrange("p (i t) -> p t i", t=4),
                    lhsT=ident_bf[:],
                    rhs=source(u)[:, :, c0:c0 + P],
                    start=True,
                    stop=True,
                )

        def copy_block(u, b):
            if b >= pe_blocks(u):
                if b == 0:
                    new_il(u)
                nc.scalar.copy(
                    out=grouped[u][:, b * 2 * SUB:(b + 1) * 2 * SUB].rearrange("p (c i t) -> p c t i", i=4, t=4),
                    in_=source(u)[:, :, b * 256:(b + 1) * 256].rearrange("p t (c i) -> p c t i", i=4),
                )
                return
            nc.scalar.copy(out=grouped[u][:, b * 2 * SUB:(b + 1) * 2 * SUB], in_=banks.pop((u, b))[:])

        tasks = []
        for u in units:
            if u[0] == "up":
                tasks += [(u, t, u[1][1]) for t in range(4)]
            tasks += [(u, b, 512 if b < pe_blocks(u) else 1060) for b in range(pe_blocks(u) + sc_blocks(u))]

        def pe_to(n):
            while state["pe"] < min(n, len(tasks)):
                u, part, cost = tasks[state["pe"]]
                state["pe"] += 1
                if u[0] == "gate" and part < pe_blocks(u):
                    pe_block(u, part)

        def s_tasks(n):
            for _ in range(n):
                if state["task"] < len(tasks):
                    pe_to(state["task"] + 1 + state["lead"])
                    u, part, cost = tasks[state["task"]]
                    state["task"] += 1
                    if u[0] == "gate":
                        copy_block(u, part)
                    else:
                        widen(u, part)

        def tasks_before(i):
            return sum(1 for t in tasks if t[0] in units[:i])

        def il(u):
            kind, (c, w), g = u
            pe = 256 * (pe_blocks(u) + sc_blocks(u))
            if pe == 0:
                new_il(u)
            if kind == "wo" and w == LW:
                for n in range(2):
                    nc.vector.tensor_copy(
                        out=grouped[u][:, n * 4 * SUB:(n + 1) * 4 * SUB].rearrange("p (c i t) -> p c t i", i=4, t=4),
                        in_=wo_raw[g][n].rearrange("p t (c i) -> p c t i", i=4),
                    )
            elif pe < w:
                nc.vector.tensor_copy(
                    out=grouped[u][:, 4 * pe:].rearrange("p (c i t) -> p c t i", i=4, t=4),
                    in_=source(u)[:, :, pe:].rearrange("p t (c i) -> p c t i", i=4),
                )

        def quant():
            u = units[state["q"]]
            state["q"] += 1
            kind, (c, w), g = u
            if kind == "wo":
                if "wo" not in codes:
                    codes["wo"] = (
                        keep.tile([P, G, LW], U32, name="wo_codes", align_bytes=64),
                        keep.tile([P, G, LW], U8, name="wo_scales", align_bytes=64),
                    )
                cd, sc = codes["wo"]
                cols = slice(c, c + w)
            else:
                if (kind, c) not in codes:
                    codes[kind, c] = (
                        work.tile([P, G, w], U32, name="codes", bufs=CODE_BUFS, align_bytes=64),
                        work.tile([P, G, w], U8, name="scales", bufs=CODE_BUFS, align_bytes=64),
                    )
                cd, sc = codes[kind, c]
                cols = slice(0, w)
            nc.vector.quantize_mx(out=cd[:, g, cols].bitcast(FP8X4), scales=sc[:, g, cols], in_=grouped.pop(u)[:])

        def load_more():
            c = state["load"]
            if c < F // LW:
                state["load"] += 1
                load_gate(0, c)
                load_up(0, c)
                load_gate(1, c)
                load_up(1, c)

        def prep():
            i = state["il"]
            if i < len(units):
                kind, (c, w), g = units[i]
                need = 1 if i < len(HEAD) else min(F // LW - 1, c // LW + 1 + (c % LW + w > LW - LOAD_LEAD))
                while state["load"] <= need:
                    load_more()
                s_tasks(tasks_before(i + 1) - state["task"])
                state["il"] += 1
                il(units[i])
            if state["q"] < state["il"] - (1 if i < len(units) else 0):
                quant()

        def v_cols():
            return sum(u[1][1] for u in units[:state["il"]])

        def s_cost():
            return sum(t[2] for t in tasks[:state["task"]])

        def turn_pe(words):
            bank = psum.tile([P, G, 2, P], F32, name="bank")
            for g in range(G):
                for u in range(2):
                    nc.tensor.transpose(bank[:, g, u, :], words[:, 256 * g + u:256 * (g + 1):2], ident[:])
            return bank

        def turn_copy(bank):
            t = work.tile([P, G * P * 4], BF16, name="turned", bufs=TURN_BUFS, align_bytes=64)
            nc.scalar.copy(
                out=t[:].bitcast(F32).rearrange("p (g r u) -> p g r u", g=G, u=2),
                in_=bank[:].rearrange("p g u r -> p g r u"),
            )
            return t

        def turn_quant(t, dst, m):
            nc.vector.quantize_mx(out=dst[0][:, m, :].bitcast(FP8X4), scales=dst[1][:, m, :], in_=t[:])

        def mm(bank, lhs, m, rhs, c, w):
            for g in range(G):
                nc.tensor.matmul_mx(
                    out=bank[:],
                    lhsT=lhs[0][:, m, g * P:(g + 1) * P].bitcast(FP8X4),
                    lhsT_scale=lhs[1][:, m, g * P:(g + 1) * P],
                    rhs=rhs[0][:, g, c:c + w].bitcast(FP8X4),
                    rhs_scale=rhs[1][:, g, c:c + w],
                    start=(g == 0),
                    stop=(g == G - 1),
                )

        at_codes = keep.tile([P, M_TILES, G * P], U32, align_bytes=64)
        at_scales = keep.tile([P, M_TILES, G * P], U8, align_bytes=64)
        at_q = (at_codes, at_scales)
        hn_codes = keep.tile([P, M_TILES, G * P], U32, align_bytes=64)
        hn_scales = keep.tile([P, M_TILES, G * P], U8, align_bytes=64)
        hn_q = (hn_codes, hn_scales)

        turned = {}
        s_tasks(S0)
        prep()
        s_tasks(SA[0])
        prep()
        for m in range(M_TILES):
            turned[m] = turn_copy(turn_pe(at_raw[m][:].bitcast(F32)))
            s_tasks(SA[m + 1])
            for n in range(NA[m]):
                prep()
            if m > 0:
                turn_quant(turned.pop(m - 1), at_q, m - 1)
        while state["q"] < n_wo:
            prep()
        turn_quant(turned.pop(3), at_q, 3)
        s2b = psum.tile([P, E], BF16, name="bank")
        for n in range(2):
            cols = slice(n * SUB, (n + 1) * SUB)
            nc.tensor.matmul(s2b[:, cols], lhsT=ones[:], rhs=s2row[:, cols], start=True, stop=True)

        h_banks = {}
        h_t = {}
        r_t = {}

        def h_mm(m):
            for n in range(2):
                h_banks[m, n] = psum.tile([P, SUB], F32, name="bank")
                mm(h_banks[m, n], at_q, m, codes["wo"], n * SUB, SUB)

        def h_add(m):
            h_t[m] = work.tile([P, E], F32, name="f4k", bufs=F4K_BUFS)
            for n in range(2):
                cols = slice(n * SUB, (n + 1) * SUB)
                nc.vector.tensor_tensor(
                    out=h_t[m][:, cols], in0=h_banks.pop((m, n))[:], in1=x_raw[m][:, cols], op=ALU.add
                )
            nc.sync.dma_start(out=h_v[m], in_=h_t[m][:])

        def h_stat(m):
            junk = work.tile([P, E], F32, name="f4k", bufs=F4K_BUFS)
            stat = work.tile([P, 8], F32, name="stat", bufs=2)
            var = work.tile([P, 8], F32, name="var", bufs=2)
            r_t[m] = work.tile([P, 8], F32, name="rstd", bufs=2)
            nc.scalar.activation(out=junk[:], in_=h_t[m][:], func=ACT.Square, scale=1.0 / 32.0, accum_out=stat[:, 0:1])
            nc.gpsimd.tensor_scalar(out=var[:, 0:1], in0=stat[:, 0:1], scalar1=1.0, scalar2=EPS, op0=ALU.mult, op1=ALU.add)
            nc.gpsimd.tensor_tensor(out=r_t[m][:, 0:1], in0=var[:, 0:1], in1=neghalf[:], op=ALU.pow)

        def h_norm(m):
            hn = work.tile([P, E], BF16, name="hn", bufs=2)
            nc.vector.scalar_tensor_tensor(
                out=hn[:], in0=h_t.pop(m)[:], scalar=r_t.pop(m)[:, 0:1], in1=s2b[:], op0=ALU.mult, op1=ALU.mult
            )
            return hn

        steps = [
            (ch, m, p0, min(SUB, ch[1])) for ch in chunks for m in range(M_TILES) for p0 in range(0, ch[1], SUB)
        ]
        gb = {}
        ub = {}
        gel = {}
        res = {}
        nxt = {"mm": 0, "gelu": 0, "mul": 0}

        def out_mm(j):
            (c, w), m, p0, pw = steps[j]
            last = max(units.index(("gate", (c, w), 1)), units.index(("up", (c, w), 1)))
            while state["q"] <= last:
                prep()
            gb[j] = psum.tile([P, pw], F32, name="bank")
            mm(gb[j], hn_q, m, codes["gate", c], p0, pw)
            ub[j] = psum.tile([P, pw], F32, name="bank")
            mm(ub[j], hn_q, m, codes["up", c], p0, pw)

        def out_gelu(j):
            gel[j] = work.tile([P, steps[j][3]], F32, name="gel", bufs=GEL_BUFS)
            nc.scalar.activation(out=gel[j][:], in_=gb.pop(j)[:], func=ACT.Gelu_apprx_tanh)

        def out_mul(j):
            (c, w), m, p0, pw = steps[j]
            if p0 == 0:
                res[m] = work.tile([P, w], F32, name="f4k", bufs=F4K_BUFS)
            nc.vector.tensor_tensor(out=res[m][:, p0:p0 + pw], in0=ub.pop(j)[:], in1=gel.pop(j)[:], op=ALU.mult)
            if p0 + pw == w:
                nc.sync.dma_start(out=act_v[m][:, c:c + w], in_=res[m][:])

        def mm_to(n):
            while nxt["mm"] < min(n, len(steps)):
                out_mm(nxt["mm"])
                nxt["mm"] += 1

        def gelu_to(n):
            mm_to(n)
            while nxt["gelu"] < min(n, len(steps)):
                out_gelu(nxt["gelu"])
                nxt["gelu"] += 1

        def mul_to(n):
            gelu_to(n)
            while nxt["mul"] < min(n, len(steps)):
                out_mul(nxt["mul"])
                nxt["mul"] += 1

        per_m = max(1, chunks[0][1] // SUB)
        state["lead"] = PE_AHEAD_B
        h_mm(0)
        h_mm(1)
        for i in range(M_TILES + 2):
            if i < M_TILES:
                h_add(i)
                h_stat(i)
            s_tasks(SC[i])
            for n in range(NB1[i]):
                prep()
            if 1 <= i <= M_TILES:
                hn = h_norm(i - 1)
                bank = turn_pe(hn[:].bitcast(F32))
            s_tasks(SD[i])
            if 1 <= i <= M_TILES:
                turned[i - 1] = turn_copy(bank)
            if i + 2 < M_TILES:
                h_mm(i + 2)
            gelu_to(per_m * (i - 2 - OL))
            for n in range(NB2[i]):
                prep()
            if 2 <= i:
                turn_quant(turned.pop(i - 2), hn_q, i - 2)
                mm_to(per_m * (i - 1 - OL))
            mul_to(per_m * (i - 3 - OL))

        state["lead"] = PE_AHEAD
        def cum(j):
            return sum(s[3] for s in steps[:j])

        v0, s0, k0 = v_cols(), s_cost(), cum(nxt["mul"])
        v_all, s_all = sum(u[1][1] for u in units), sum(t[2] for t in tasks)
        for j in range(nxt["mul"], len(steps)):
            done = cum(j + 1) - k0
            mm_to(j + ML)
            n = state["task"]
            want = s0 + (s_all - s0) * done / (LAST_S * 512 - k0)
            while state["task"] < len(tasks) and s_cost() + tasks[state["task"]][2] / 2 < want:
                s_tasks(1)
                if state["task"] == n + 1:
                    gelu_to(j + GL)
            gelu_to(j + GL)
            want = v0 + (v_all - v0) * done / (LAST * 512 - k0)
            while state["il"] < len(units) and v_cols() + units[state["il"]][1][1] / 2 < want:
                prep()
            if state["il"] == len(units) and state["q"] < len(units):
                prep()
            mm_to(j + ML + M2)
            mul_to(j + 1)
